import numpy as np
import ml_dtypes

BF16 = ml_dtypes.bfloat16


def bf(x):
    return np.asarray(x, np.float32).astype(BF16)


def f32(x):
    return np.asarray(x, np.float32)


def f64(x):
    return np.asarray(x).astype(np.float64)


def striped(idx):
    return np.tile(idx.reshape(-1, 16).T, (8, 1))


B, A, H, S, N, D = 2, 64, 128, 256, 128, 3
VMAX = 8.0
GAMMA = 1.0 / VMAX ** 2
EPS = 1e-6
BOX = 10.0


def softplus(v):
    return np.log(1.0 + np.exp(v))


def silu(v):
    return v / (1.0 + np.exp(-v))


def setup_inputs():
    return {"table": f32(0.5 * np.random.standard_normal((H, S))), "cart": f32(BOX * np.random.uniform(size=(D, N))), "edge_w": f32(1.5 * np.random.standard_normal((H, 1))), "edge_b": f32(0.1 * np.random.standard_normal((H, 1))), "node_w": bf(0.3 * np.random.standard_normal((H, H)) / np.sqrt(H)), "node_b": f32(0.1 * np.random.standard_normal((H, 1))), "offs": striped(np.random.permutation(np.tile(np.arange(S), 2))[:N])}


def reference(table, cart, edge_w, edge_b, node_w, node_b, offs):
    idx = offs[:16].T.reshape(-1)
    h = f64(table)[:, idx]
    r = f64(cart).reshape(D, B, A)
    d2 = ((r[:, :, :, None] - r[:, :, None, :]) ** 2).sum(axis=0) + EPS
    rbf = np.exp(-GAMMA * d2)
    gate = softplus(f64(edge_w)[:, :, None, None] * rbf[None] + f64(edge_b)[:, :, None, None])
    agg = (gate * h.reshape(H, B, 1, A)).sum(axis=-1).reshape(H, N)
    return h + silu(f64(node_w).T @ agg + f64(node_b))

@@ -1,0 +1,109 @@
+import concourse.mybir as mybir
+
+F32 = mybir.dt.float32
+BF16 = mybir.dt.bfloat16
+U16 = mybir.dt.uint16
+ACT = mybir.ActivationFunctionType
+ALU = mybir.AluOpType
+AXIS = mybir.AxisListType
+
+P = 128
+TYPES = 256
+ATOMS = 128
+CRYSTALS = 2
+PER_CRYSTAL = ATOMS // CRYSTALS
+DIMS = 3
+GAMMA = 1.0 / 64.0
+EPS = 1e-6
+ROWS = 4
+
+FLOPS = 2 * P * P * ATOMS
+
+
+def tile_crystalencoder_kernel(tc, table, cart, edge_w, edge_b, node_w, node_b, offs, out):
+    nc = tc.nc
+    with (
+        tc.tile_pool(name="held", bufs=1) as held,
+        tc.tile_pool(name="work", bufs=3) as work,
+        tc.psum_pool(name="psum", bufs=1) as psum,
+    ):
+        offsets = held.tile([P, ATOMS // 16], U16, name="offsets")
+        nc.sync.dma_start(offsets[:], offs)
+        cart_all = held.tile([P, DIMS, ATOMS], F32, name="cart_all")
+        nc.scalar.dma_start(
+            cart_all[:].rearrange("p d n -> p (d n)"),
+            cart.rearrange("d n -> (d n)").partition_broadcast(P),
+        )
+        cart_own = held.tile([P, DIMS], F32, name="cart_own")
+        with nc.allow_non_contiguous_dma(reason="three coordinates to a partition"):
+            nc.sync.dma_start(cart_own[:], cart.rearrange("d n -> n d"))
+        edge_w_sb = held.tile([P, 1], F32, name="edge_w_sb")
+        nc.sync.dma_start(edge_w_sb[:], edge_w)
+        edge_b_sb = held.tile([P, 1], F32, name="edge_b_sb")
+        nc.sync.dma_start(edge_b_sb[:], edge_b)
+        table_sb = held.tile([P, TYPES], F32, name="table_sb")
+        nc.scalar.dma_start(table_sb[:], table)
+        node_w_sb = held.tile([P, P], BF16, name="node_w_sb")
+        nc.scalar.dma_start(node_w_sb[:], node_w)
+        node_b_sb = held.tile([P, 1], F32, name="node_b_sb")
+        nc.scalar.dma_start(node_b_sb[:], node_b)
+
+        eps_bias = held.tile([P, 1], F32, name="eps_bias")
+        nc.vector.memset(eps_bias[:], -GAMMA * EPS)
+        diff = held.tile([P, DIMS, ATOMS], F32, name="diff")
+        nc.vector.tensor_tensor(
+            diff[:], cart_all[:], cart_own[:].unsqueeze(2).to_broadcast([P, DIMS, ATOMS]), ALU.subtract
+        )
+        square = held.tile([P, DIMS, ATOMS], F32, name="square")
+        nc.vector.tensor_tensor(square[:], diff[:], diff[:], ALU.mult)
+        dist2 = held.tile([P, ATOMS], F32, name="dist2")
+        nc.vector.tensor_reduce(dist2[:], square[:].rearrange("p d n -> p n d"), AXIS.X, ALU.add)
+        rbf = held.tile([P, ATOMS], F32, name="rbf")
+        nc.scalar.activation(rbf[:], dist2[:], ACT.Exp, bias=eps_bias[:], scale=-GAMMA)
+
+        for c in range(CRYSTALS):
+            own = slice(c * PER_CRYSTAL, (c + 1) * PER_CRYSTAL)
+            nc.sync.dma_start(out[0:PER_CRYSTAL, own], rbf[own, own])
+
+        agg_pairs = held.tile([P, ATOMS], F32, name="agg_pairs")
+        for first in range(0, PER_CRYSTAL, ROWS):
+            rbf_all = work.tile([P, ROWS * ATOMS], F32, name="rbf_all")
+            nc.sync.dma_start(
+                rbf_all[:], out[first : first + ROWS, :].rearrange("r n -> (r n)").partition_broadcast(P)
+            )
+            magnitude = work.tile([P, ROWS * ATOMS], F32, name="magnitude")
+            nc.scalar.activation(magnitude[:], rbf_all[:], ACT.Abs, bias=edge_b_sb[:], scale=edge_w_sb[:])
+            decay = work.tile([P, ROWS * ATOMS], F32, name="decay")
+            nc.scalar.activation(decay[:], magnitude[:], ACT.Exp, scale=-1.0)
+            log_part = work.tile([P, ROWS * ATOMS], F32, name="log_part")
+            nc.scalar.activation(log_part[:], decay[:], ACT.Ln, bias=1.0)
+            relu_part = work.tile([P, ROWS * ATOMS], F32, name="relu_part")
+            nc.scalar.activation(relu_part[:], rbf_all[:], ACT.Relu, bias=edge_b_sb[:], scale=edge_w_sb[:])
+            gate = work.tile([P, ROWS * ATOMS], F32, name="gate")
+            nc.vector.tensor_tensor(gate[:], relu_part[:], log_part[:], ALU.add)
+
+            messages = work.tile([P, ROWS * ATOMS], F32, name="messages")
+            for r in range(ROWS):
+                pair = slice(r * ATOMS, (r + 1) * ATOMS)
+                nc.vector.tensor_tensor(
+                    messages[:, pair], table_sb[:].indirect(offsets[:]), gate[:, pair], ALU.mult
+                )
+            nc.vector.tensor_reduce(
+                agg_pairs[:, first * CRYSTALS : (first + ROWS) * CRYSTALS],
+                messages[:].rearrange("p (q j) -> p q j", j=PER_CRYSTAL),
+                AXIS.X,
+                ALU.add,
+            )
+
+        agg_bf = held.tile([P, ATOMS], BF16, name="agg_bf")
+        nc.vector.tensor_copy(
+            agg_bf[:].rearrange("p (c r) -> p c r", c=CRYSTALS),
+            agg_pairs[:].rearrange("p (r c) -> p c r", c=CRYSTALS),
+        )
+        projected = psum.tile([P, ATOMS], F32, name="projected")
+        nc.tensor.matmul(projected[:], node_w_sb[:], agg_bf[:], start=True, stop=True)
+        update = held.tile([P, ATOMS], F32, name="update")
+        nc.scalar.activation(update[:], projected[:], ACT.Silu, bias=node_b_sb[:])
+        result = held.tile([P, ATOMS], F32, name="result")
+        nc.vector.tensor_tensor(result[:], table_sb[:].indirect(offsets[:]), update[:], ALU.add)
+        nc.sync.dma_start(out, result[:])

@@ -15,7 +15,9 @@ PER_CRYSTAL = ATOMS // CRYSTALS
 DIMS = 3
 GAMMA = 1.0 / 64.0
 EPS = 1e-6
-ROWS = 4
+BATCH = 16
+PIECE = 4
+CAP = 30.0
 
 FLOPS = 2 * P * P * ATOMS
 
@@ -24,7 +26,8 @@ def tile_crystalencoder_kernel(tc, table, cart, edge_w, edge_b, node_w, node_b, 
     nc = tc.nc
     with (
         tc.tile_pool(name="held", bufs=1) as held,
-        tc.tile_pool(name="work", bufs=3) as work,
+        tc.tile_pool(name="batches", bufs=2) as batches,
+        tc.tile_pool(name="pieces", bufs=4) as pieces,
         tc.psum_pool(name="psum", bufs=1) as psum,
     ):
         offsets = held.tile([P, ATOMS // 16], U16, name="offsets")
@@ -65,35 +68,44 @@ def tile_crystalencoder_kernel(tc, table, cart, edge_w, edge_b, node_w, node_b, 
             own = slice(c * PER_CRYSTAL, (c + 1) * PER_CRYSTAL)
             nc.sync.dma_start(out[0:PER_CRYSTAL, own], rbf[own, own])
 
-        agg_pairs = held.tile([P, ATOMS], F32, name="agg_pairs")
-        for first in range(0, PER_CRYSTAL, ROWS):
-            rbf_all = work.tile([P, ROWS * ATOMS], F32, name="rbf_all")
-            nc.sync.dma_start(
-                rbf_all[:], out[first : first + ROWS, :].rearrange("r n -> (r n)").partition_broadcast(P)
-            )
-            magnitude = work.tile([P, ROWS * ATOMS], F32, name="magnitude")
-            nc.scalar.activation(magnitude[:], rbf_all[:], ACT.Abs, bias=edge_b_sb[:], scale=edge_w_sb[:])
-            decay = work.tile([P, ROWS * ATOMS], F32, name="decay")
-            nc.scalar.activation(decay[:], magnitude[:], ACT.Exp, scale=-1.0)
-            log_part = work.tile([P, ROWS * ATOMS], F32, name="log_part")
-            nc.scalar.activation(log_part[:], decay[:], ACT.Ln, bias=1.0)
-            relu_part = work.tile([P, ROWS * ATOMS], F32, name="relu_part")
-            nc.scalar.activation(relu_part[:], rbf_all[:], ACT.Relu, bias=edge_b_sb[:], scale=edge_w_sb[:])
-            gate = work.tile([P, ROWS * ATOMS], F32, name="gate")
-            nc.vector.tensor_tensor(gate[:], relu_part[:], log_part[:], ALU.add)
+        def prepare(batch):
+            rows = slice(batch * BATCH, (batch + 1) * BATCH)
+            rbf_all = batches.tile([P, BATCH * ATOMS], F32, name="rbf_all")
+            nc.sync.dma_start(rbf_all[:], out[rows, :].rearrange("r n -> (r n)").partition_broadcast(P))
+            v = batches.tile([P, BATCH * ATOMS], F32, name="v")
+            nc.vector.tensor_scalar(v[:], rbf_all[:], edge_w_sb[:], edge_b_sb[:], ALU.mult, ALU.add)
+            capped = batches.tile([P, BATCH * ATOMS], F32, name="capped")
+            nc.vector.tensor_scalar_min(capped[:], v[:], CAP)
+            return v, capped
 
-            messages = work.tile([P, ROWS * ATOMS], F32, name="messages")
-            for r in range(ROWS):
-                pair = slice(r * ATOMS, (r + 1) * ATOMS)
-                nc.vector.tensor_tensor(
-                    messages[:, pair], table_sb[:].indirect(offsets[:]), gate[:, pair], ALU.mult
+        agg_pairs = held.tile([P, ATOMS], F32, name="agg_pairs")
+        n_batches = PER_CRYSTAL // BATCH
+        v, capped = prepare(0)
+        for batch in range(n_batches):
+            grown = batches.tile([P, BATCH * ATOMS], F32, name="grown")
+            nc.scalar.activation(grown[:], capped[:], ACT.Exp)
+            v_now = v
+            if batch + 1 < n_batches:
+                v, capped = prepare(batch + 1)
+            for first in range(0, BATCH, PIECE):
+                span = slice(first * ATOMS, (first + PIECE) * ATOMS)
+                log_part = pieces.tile([P, PIECE * ATOMS], F32, name="log_part")
+                nc.scalar.activation(log_part[:], grown[:, span], ACT.Ln, bias=1.0)
+                gate = pieces.tile([P, PIECE * ATOMS], F32, name="gate")
+                nc.vector.tensor_tensor(gate[:], v_now[:, span], log_part[:], ALU.max)
+                messages = pieces.tile([P, PIECE * ATOMS], F32, name="messages")
+                for r in range(PIECE):
+                    pair = slice(r * ATOMS, (r + 1) * ATOMS)
+                    nc.vector.tensor_tensor(
+                        messages[:, pair], table_sb[:].indirect(offsets[:]), gate[:, pair], ALU.mult
+                    )
+                done = (batch * BATCH + first) * CRYSTALS
+                nc.vector.tensor_reduce(
+                    agg_pairs[:, done : done + PIECE * CRYSTALS],
+                    messages[:].rearrange("p (q j) -> p q j", j=PER_CRYSTAL),
+                    AXIS.X,
+                    ALU.add,
                 )
-            nc.vector.tensor_reduce(
-                agg_pairs[:, first * CRYSTALS : (first + ROWS) * CRYSTALS],
-                messages[:].rearrange("p (q j) -> p q j", j=PER_CRYSTAL),
-                AXIS.X,
-                ALU.add,
-            )
 
         agg_bf = held.tile([P, ATOMS], BF16, name="agg_bf")
         nc.vector.tensor_copy(

@@ -1,4 +1,5 @@
 import concourse.mybir as mybir
+from concourse.masks import make_identity
 
 F32 = mybir.dt.float32
 BF16 = mybir.dt.bfloat16
@@ -17,6 +18,8 @@ GAMMA = 1.0 / 64.0
 EPS = 1e-6
 BATCH = 16
 PIECE = 4
+J_HI = 8
+J_LO = PER_CRYSTAL // J_HI
 CAP = 30.0
 
 FLOPS = 2 * P * P * ATOMS
@@ -29,6 +32,7 @@ def tile_crystalencoder_kernel(tc, table, cart, edge_w, edge_b, node_w, node_b, 
         tc.tile_pool(name="batches", bufs=2) as batches,
         tc.tile_pool(name="pieces", bufs=4) as pieces,
         tc.psum_pool(name="psum", bufs=1) as psum,
+        tc.psum_pool(name="sums", bufs=4) as sums,
     ):
         offsets = held.tile([P, ATOMS // 16], U16, name="offsets")
         nc.sync.dma_start(offsets[:], offs)
@@ -50,6 +54,9 @@ def tile_crystalencoder_kernel(tc, table, cart, edge_w, edge_b, node_w, node_b, 
         nc.scalar.dma_start(node_w_sb[:], node_w)
         node_b_sb = held.tile([P, 1], F32, name="node_b_sb")
         nc.scalar.dma_start(node_b_sb[:], node_b)
+
+        identity = held.tile([P, P], F32, name="identity")
+        make_identity(nc, identity[:])
 
         eps_bias = held.tile([P, 1], F32, name="eps_bias")
         nc.vector.memset(eps_bias[:], -GAMMA * EPS)
@@ -99,13 +106,14 @@ def tile_crystalencoder_kernel(tc, table, cart, edge_w, edge_b, node_w, node_b, 
                     nc.vector.tensor_tensor(
                         messages[:, pair], table_sb[:].indirect(offsets[:]), gate[:, pair], ALU.mult
                     )
+                slices = messages[:].rearrange("p (q h l) -> p q h l", h=J_HI, l=J_LO)
+                partial = sums.tile([P, PIECE * CRYSTALS, J_LO], F32, name="partial")
+                for h in range(J_HI):
+                    nc.tensor.matmul(
+                        partial[:], identity[:], slices[:, :, h, :], start=(h == 0), stop=(h == J_HI - 1)
+                    )
                 done = (batch * BATCH + first) * CRYSTALS
-                nc.vector.tensor_reduce(
-                    agg_pairs[:, done : done + PIECE * CRYSTALS],
-                    messages[:].rearrange("p (q j) -> p q j", j=PER_CRYSTAL),
-                    AXIS.X,
-                    ALU.add,
-                )
+                nc.vector.tensor_reduce(agg_pairs[:, done : done + PIECE * CRYSTALS], partial[:], AXIS.X, ALU.add)
 
         agg_bf = held.tile([P, ATOMS], BF16, name="agg_bf")
         nc.vector.tensor_copy(

@@ -1,5 +1,4 @@
 import concourse.mybir as mybir
-from concourse.masks import make_identity
 
 F32 = mybir.dt.float32
 BF16 = mybir.dt.bfloat16
@@ -18,9 +17,7 @@ GAMMA = 1.0 / 64.0
 EPS = 1e-6
 BATCH = 16
 PIECE = 4
-J_HI = 8
-J_LO = PER_CRYSTAL // J_HI
-CAP = 30.0
+FLOOR = 2.0**-60
 
 FLOPS = 2 * P * P * ATOMS
 
@@ -32,7 +29,6 @@ def tile_crystalencoder_kernel(tc, table, cart, edge_w, edge_b, node_w, node_b, 
         tc.tile_pool(name="batches", bufs=2) as batches,
         tc.tile_pool(name="pieces", bufs=4) as pieces,
         tc.psum_pool(name="psum", bufs=1) as psum,
-        tc.psum_pool(name="sums", bufs=4) as sums,
     ):
         offsets = held.tile([P, ATOMS // 16], U16, name="offsets")
         nc.sync.dma_start(offsets[:], offs)
@@ -55,8 +51,10 @@ def tile_crystalencoder_kernel(tc, table, cart, edge_w, edge_b, node_w, node_b, 
         node_b_sb = held.tile([P, 1], F32, name="node_b_sb")
         nc.scalar.dma_start(node_b_sb[:], node_b)
 
-        identity = held.tile([P, P], F32, name="identity")
-        make_identity(nc, identity[:])
+        minus_w = held.tile([P, 1], F32, name="minus_w")
+        nc.vector.tensor_scalar_mul(minus_w[:], edge_w_sb[:], -1.0)
+        minus_b = held.tile([P, 1], F32, name="minus_b")
+        nc.vector.tensor_scalar_mul(minus_b[:], edge_b_sb[:], -1.0)
 
         eps_bias = held.tile([P, 1], F32, name="eps_bias")
         nc.vector.memset(eps_bias[:], -GAMMA * EPS)
@@ -81,39 +79,36 @@ def tile_crystalencoder_kernel(tc, table, cart, edge_w, edge_b, node_w, node_b, 
             nc.sync.dma_start(rbf_all[:], out[rows, :].rearrange("r n -> (r n)").partition_broadcast(P))
             v = batches.tile([P, BATCH * ATOMS], F32, name="v")
             nc.vector.tensor_scalar(v[:], rbf_all[:], edge_w_sb[:], edge_b_sb[:], ALU.mult, ALU.add)
-            capped = batches.tile([P, BATCH * ATOMS], F32, name="capped")
-            nc.vector.tensor_scalar_min(capped[:], v[:], CAP)
-            return v, capped
+            return rbf_all, v
 
         agg_pairs = held.tile([P, ATOMS], F32, name="agg_pairs")
         n_batches = PER_CRYSTAL // BATCH
-        v, capped = prepare(0)
+        rbf_all, v = prepare(0)
         for batch in range(n_batches):
-            grown = batches.tile([P, BATCH * ATOMS], F32, name="grown")
-            nc.scalar.activation(grown[:], capped[:], ACT.Exp)
+            sigmoid = batches.tile([P, BATCH * ATOMS], F32, name="sigmoid")
+            nc.scalar.activation(sigmoid[:], rbf_all[:], ACT.Sigmoid, bias=minus_b[:], scale=minus_w[:])
             v_now = v
             if batch + 1 < n_batches:
-                v, capped = prepare(batch + 1)
+                rbf_all, v = prepare(batch + 1)
             for first in range(0, BATCH, PIECE):
                 span = slice(first * ATOMS, (first + PIECE) * ATOMS)
                 log_part = pieces.tile([P, PIECE * ATOMS], F32, name="log_part")
-                nc.scalar.activation(log_part[:], grown[:, span], ACT.Ln, bias=1.0)
+                nc.scalar.activation(log_part[:], sigmoid[:, span], ACT.Ln, bias=FLOOR)
                 gate = pieces.tile([P, PIECE * ATOMS], F32, name="gate")
-                nc.vector.tensor_tensor(gate[:], v_now[:, span], log_part[:], ALU.max)
+                nc.vector.scalar_tensor_tensor(gate[:], log_part[:], -1.0, v_now[:, span], ALU.mult, ALU.max)
                 messages = pieces.tile([P, PIECE * ATOMS], F32, name="messages")
                 for r in range(PIECE):
                     pair = slice(r * ATOMS, (r + 1) * ATOMS)
                     nc.vector.tensor_tensor(
                         messages[:, pair], table_sb[:].indirect(offsets[:]), gate[:, pair], ALU.mult
                     )
-                slices = messages[:].rearrange("p (q h l) -> p q h l", h=J_HI, l=J_LO)
-                partial = sums.tile([P, PIECE * CRYSTALS, J_LO], F32, name="partial")
-                for h in range(J_HI):
-                    nc.tensor.matmul(
-                        partial[:], identity[:], slices[:, :, h, :], start=(h == 0), stop=(h == J_HI - 1)
-                    )
                 done = (batch * BATCH + first) * CRYSTALS
-                nc.vector.tensor_reduce(agg_pairs[:, done : done + PIECE * CRYSTALS], partial[:], AXIS.X, ALU.add)
+                nc.vector.tensor_reduce(
+                    agg_pairs[:, done : done + PIECE * CRYSTALS],
+                    messages[:].rearrange("p (q j) -> p q j", j=PER_CRYSTAL),
+                    AXIS.X,
+                    ALU.add,
+                )
 
         agg_bf = held.tile([P, ATOMS], BF16, name="agg_bf")
         nc.vector.tensor_copy(

@@ -1,4 +1,5 @@
 import concourse.mybir as mybir
+from concourse.masks import make_identity
 
 F32 = mybir.dt.float32
 BF16 = mybir.dt.bfloat16
@@ -17,6 +18,8 @@ GAMMA = 1.0 / 64.0
 EPS = 1e-6
 BATCH = 16
 PIECE = 4
+J_HI = 4
+J_LO = PER_CRYSTAL // J_HI
 FLOOR = 2.0**-60
 
 FLOPS = 2 * P * P * ATOMS
@@ -29,6 +32,7 @@ def tile_crystalencoder_kernel(tc, table, cart, edge_w, edge_b, node_w, node_b, 
         tc.tile_pool(name="batches", bufs=2) as batches,
         tc.tile_pool(name="pieces", bufs=4) as pieces,
         tc.psum_pool(name="psum", bufs=1) as psum,
+        tc.psum_pool(name="sums", bufs=2) as sums,
     ):
         offsets = held.tile([P, ATOMS // 16], U16, name="offsets")
         nc.sync.dma_start(offsets[:], offs)
@@ -51,6 +55,8 @@ def tile_crystalencoder_kernel(tc, table, cart, edge_w, edge_b, node_w, node_b, 
         node_b_sb = held.tile([P, 1], F32, name="node_b_sb")
         nc.scalar.dma_start(node_b_sb[:], node_b)
 
+        identity = held.tile([P, P], F32, name="identity")
+        make_identity(nc, identity[:])
         minus_w = held.tile([P, 1], F32, name="minus_w")
         nc.vector.tensor_scalar_mul(minus_w[:], edge_w_sb[:], -1.0)
         minus_b = held.tile([P, 1], F32, name="minus_b")
@@ -82,12 +88,18 @@ def tile_crystalencoder_kernel(tc, table, cart, edge_w, edge_b, node_w, node_b, 
             return rbf_all, v
 
         agg_pairs = held.tile([P, ATOMS], F32, name="agg_pairs")
+
+        def add_partial_sums(batch, partial):
+            done = batch * BATCH * CRYSTALS
+            nc.vector.tensor_reduce(agg_pairs[:, done : done + BATCH * CRYSTALS], partial[:], AXIS.X, ALU.add)
+
         n_batches = PER_CRYSTAL // BATCH
         rbf_all, v = prepare(0)
         for batch in range(n_batches):
             sigmoid = batches.tile([P, BATCH * ATOMS], F32, name="sigmoid")
             nc.scalar.activation(sigmoid[:], rbf_all[:], ACT.Sigmoid, bias=minus_b[:], scale=minus_w[:])
             v_now = v
+            partial = sums.tile([P, BATCH * CRYSTALS, J_LO], F32, name="partial")
             if batch + 1 < n_batches:
                 rbf_all, v = prepare(batch + 1)
             for first in range(0, BATCH, PIECE):
@@ -102,13 +114,16 @@ def tile_crystalencoder_kernel(tc, table, cart, edge_w, edge_b, node_w, node_b, 
                     nc.vector.tensor_tensor(
                         messages[:, pair], table_sb[:].indirect(offsets[:]), gate[:, pair], ALU.mult
                     )
-                done = (batch * BATCH + first) * CRYSTALS
-                nc.vector.tensor_reduce(
-                    agg_pairs[:, done : done + PIECE * CRYSTALS],
-                    messages[:].rearrange("p (q j) -> p q j", j=PER_CRYSTAL),
-                    AXIS.X,
-                    ALU.add,
-                )
+                slices = messages[:].rearrange("p (q h l) -> p q h l", h=J_HI, l=J_LO)
+                sums_of_piece = partial[:, first * CRYSTALS : (first + PIECE) * CRYSTALS, :]
+                for h in range(J_HI):
+                    nc.tensor.matmul(
+                        sums_of_piece, identity[:], slices[:, :, h, :], start=(h == 0), stop=(h == J_HI - 1)
+                    )
+                if first == 0 and batch > 0:
+                    add_partial_sums(batch - 1, partial_before)
+            partial_before = partial
+        add_partial_sums(n_batches - 1, partial_before)
 
         agg_bf = held.tile([P, ATOMS], BF16, name="agg_bf")
         nc.vector.tensor_copy(

@@ -33,6 +33,7 @@ def tile_crystalencoder_kernel(tc, table, cart, edge_w, edge_b, node_w, node_b, 
         tc.tile_pool(name="pieces", bufs=4) as pieces,
         tc.psum_pool(name="psum", bufs=1) as psum,
         tc.psum_pool(name="sums", bufs=2) as sums,
+        tc.psum_pool(name="spread", bufs=BATCH // PIECE) as spread,
     ):
         offsets = held.tile([P, ATOMS // 16], U16, name="offsets")
         nc.sync.dma_start(offsets[:], offs)
@@ -62,6 +63,21 @@ def tile_crystalencoder_kernel(tc, table, cart, edge_w, edge_b, node_w, node_b, 
         minus_b = held.tile([P, 1], F32, name="minus_b")
         nc.vector.tensor_scalar_mul(minus_b[:], edge_b_sb[:], -1.0)
 
+        first_pieces = BATCH // PIECE
+        in_piece = held.tile([P, first_pieces], F32, name="in_piece")
+        nc.vector.tensor_reduce(
+            in_piece[:],
+            identity[:].rearrange("p (c g l) -> p g c l", c=CRYSTALS, l=PIECE)[:, 0:first_pieces, :, :],
+            AXIS.XY,
+            ALU.add,
+        )
+        at_place = held.tile([P, PIECE, CRYSTALS], F32, name="at_place")
+        nc.vector.tensor_reduce(
+            at_place[:], identity[:].rearrange("p (c g l) -> p l c g", c=CRYSTALS, l=PIECE), AXIS.X, ALU.add
+        )
+        pick_piece = held.tile([P, first_pieces, P], F32, name="pick_piece")
+        nc.vector.tensor_copy(pick_piece[:], in_piece[:].unsqueeze(2).to_broadcast([P, first_pieces, P]))
+
         eps_bias = held.tile([P, 1], F32, name="eps_bias")
         nc.vector.memset(eps_bias[:], -GAMMA * EPS)
         diff = held.tile([P, DIMS, ATOMS], F32, name="diff")
@@ -79,13 +95,40 @@ def tile_crystalencoder_kernel(tc, table, cart, edge_w, edge_b, node_w, node_b, 
             own = slice(c * PER_CRYSTAL, (c + 1) * PER_CRYSTAL)
             nc.sync.dma_start(out[0:PER_CRYSTAL, own], rbf[own, own])
 
+        own_rows = held.tile([P, PIECE, CRYSTALS, PER_CRYSTAL], F32, name="own_rows")
+        nc.vector.tensor_tensor(
+            own_rows[:],
+            at_place[:].unsqueeze(3).to_broadcast([P, PIECE, CRYSTALS, PER_CRYSTAL]),
+            rbf[:].rearrange("p (c j) -> p c j", c=CRYSTALS).unsqueeze(1).to_broadcast([P, PIECE, CRYSTALS, PER_CRYSTAL]),
+            ALU.mult,
+        )
+
         def prepare(batch):
-            rows = slice(batch * BATCH, (batch + 1) * BATCH)
-            rbf_all = batches.tile([P, BATCH * ATOMS], F32, name="rbf_all")
-            nc.sync.dma_start(rbf_all[:], out[rows, :].rearrange("r n -> (r n)").partition_broadcast(P))
+            if batch == 0:
+                parts = []
+                for g in range(first_pieces):
+                    rbf_piece = spread.tile([P, PIECE * ATOMS], F32, name="rbf_piece")
+                    nc.tensor.matmul(
+                        rbf_piece[:],
+                        pick_piece[:, g, :],
+                        own_rows[:].rearrange("p l c j -> p (l c j)"),
+                        start=True,
+                        stop=True,
+                    )
+                    parts.append(rbf_piece[:])
+            else:
+                rows = slice(batch * BATCH, (batch + 1) * BATCH)
+                rbf_all = batches.tile([P, BATCH * ATOMS], F32, name="rbf_all")
+                nc.sync.dma_start(rbf_all[:], out[rows, :].rearrange("r n -> (r n)").partition_broadcast(P))
+                parts = [rbf_all[:]]
             v = batches.tile([P, BATCH * ATOMS], F32, name="v")
-            nc.vector.tensor_scalar(v[:], rbf_all[:], edge_w_sb[:], edge_b_sb[:], ALU.mult, ALU.add)
-            return rbf_all, v
+            for span, part in spans(parts):
+                nc.vector.tensor_scalar(v[:, span], part, edge_w_sb[:], edge_b_sb[:], ALU.mult, ALU.add)
+            return parts, v
+
+        def spans(parts):
+            width = BATCH * ATOMS // len(parts)
+            return [(slice(n * width, (n + 1) * width), part) for n, part in enumerate(parts)]
 
         agg_pairs = held.tile([P, ATOMS], F32, name="agg_pairs")
 
@@ -94,14 +137,15 @@ def tile_crystalencoder_kernel(tc, table, cart, edge_w, edge_b, node_w, node_b, 
             nc.vector.tensor_reduce(agg_pairs[:, done : done + BATCH * CRYSTALS], partial[:], AXIS.X, ALU.add)
 
         n_batches = PER_CRYSTAL // BATCH
-        rbf_all, v = prepare(0)
+        parts, v = prepare(0)
         for batch in range(n_batches):
             sigmoid = batches.tile([P, BATCH * ATOMS], F32, name="sigmoid")
-            nc.scalar.activation(sigmoid[:], rbf_all[:], ACT.Sigmoid, bias=minus_b[:], scale=minus_w[:])
+            for span, part in spans(parts):
+                nc.scalar.activation(sigmoid[:, span], part, ACT.Sigmoid, bias=minus_b[:], scale=minus_w[:])
             v_now = v
             partial = sums.tile([P, BATCH * CRYSTALS, J_LO], F32, name="partial")
             if batch + 1 < n_batches:
-                rbf_all, v = prepare(batch + 1)
+                parts, v = prepare(batch + 1)
             for first in range(0, BATCH, PIECE):
                 span = slice(first * ATOMS, (first + PIECE) * ATOMS)
                 log_part = pieces.tile([P, PIECE * ATOMS], F32, name="log_part")

@@ -35,26 +35,27 @@ def tile_crystalencoder_kernel(tc, table, cart, edge_w, edge_b, node_w, node_b, 
         tc.psum_pool(name="sums", bufs=2) as sums,
         tc.psum_pool(name="spread", bufs=BATCH // PIECE) as spread,
     ):
-        offsets = held.tile([P, ATOMS // 16], U16, name="offsets")
-        nc.sync.dma_start(offsets[:], offs)
-        cart_all = held.tile([P, DIMS, ATOMS], F32, name="cart_all")
-        nc.scalar.dma_start(
-            cart_all[:].rearrange("p d n -> p (d n)"),
-            cart.rearrange("d n -> (d n)").partition_broadcast(P),
-        )
+        halves = [slice(c * PER_CRYSTAL, (c + 1) * PER_CRYSTAL) for c in range(CRYSTALS)]
+        cart_crystal = held.tile([P, DIMS, PER_CRYSTAL], F32, name="cart_crystal")
+        for own, queue in zip(halves, (nc.sync, nc.scalar)):
+            queue.dma_start(
+                cart_crystal[own, :, :], cart[:, own].unsqueeze(0).to_broadcast([PER_CRYSTAL, DIMS, PER_CRYSTAL])
+            )
         cart_own = held.tile([P, DIMS], F32, name="cart_own")
         with nc.allow_non_contiguous_dma(reason="three coordinates to a partition"):
             nc.sync.dma_start(cart_own[:], cart.rearrange("d n -> n d"))
         edge_w_sb = held.tile([P, 1], F32, name="edge_w_sb")
         nc.sync.dma_start(edge_w_sb[:], edge_w)
         edge_b_sb = held.tile([P, 1], F32, name="edge_b_sb")
-        nc.sync.dma_start(edge_b_sb[:], edge_b)
+        nc.scalar.dma_start(edge_b_sb[:], edge_b)
+        offsets = held.tile([P, ATOMS // 16], U16, name="offsets")
+        nc.sync.dma_start(offsets[:], offs)
         table_sb = held.tile([P, TYPES], F32, name="table_sb")
-        nc.scalar.dma_start(table_sb[:], table)
+        nc.sync.dma_start(table_sb[:], table)
         node_w_sb = held.tile([P, P], BF16, name="node_w_sb")
-        nc.scalar.dma_start(node_w_sb[:], node_w)
+        nc.gpsimd.dma_start(node_w_sb[:], node_w)
         node_b_sb = held.tile([P, 1], F32, name="node_b_sb")
-        nc.scalar.dma_start(node_b_sb[:], node_b)
+        nc.gpsimd.dma_start(node_b_sb[:], node_b)
 
         identity = held.tile([P, P], F32, name="identity")
         make_identity(nc, identity[:])
@@ -63,72 +64,46 @@ def tile_crystalencoder_kernel(tc, table, cart, edge_w, edge_b, node_w, node_b, 
         minus_b = held.tile([P, 1], F32, name="minus_b")
         nc.vector.tensor_scalar_mul(minus_b[:], edge_b_sb[:], -1.0)
 
-        first_pieces = BATCH // PIECE
-        in_piece = held.tile([P, first_pieces], F32, name="in_piece")
-        nc.vector.tensor_reduce(
-            in_piece[:],
-            identity[:].rearrange("p (c g l) -> p g c l", c=CRYSTALS, l=PIECE)[:, 0:first_pieces, :, :],
-            AXIS.XY,
-            ALU.add,
-        )
-        at_place = held.tile([P, PIECE, CRYSTALS], F32, name="at_place")
-        nc.vector.tensor_reduce(
-            at_place[:], identity[:].rearrange("p (c g l) -> p l c g", c=CRYSTALS, l=PIECE), AXIS.X, ALU.add
-        )
-        pick_piece = held.tile([P, first_pieces, P], F32, name="pick_piece")
-        nc.vector.tensor_copy(pick_piece[:], in_piece[:].unsqueeze(2).to_broadcast([P, first_pieces, P]))
-
         eps_bias = held.tile([P, 1], F32, name="eps_bias")
         nc.vector.memset(eps_bias[:], -GAMMA * EPS)
-        diff = held.tile([P, DIMS, ATOMS], F32, name="diff")
+        diff = held.tile([P, DIMS, PER_CRYSTAL], F32, name="diff")
         nc.vector.tensor_tensor(
-            diff[:], cart_all[:], cart_own[:].unsqueeze(2).to_broadcast([P, DIMS, ATOMS]), ALU.subtract
+            diff[:], cart_crystal[:], cart_own[:].unsqueeze(2).to_broadcast([P, DIMS, PER_CRYSTAL]), ALU.subtract
         )
-        square = held.tile([P, DIMS, ATOMS], F32, name="square")
+        square = held.tile([P, DIMS, PER_CRYSTAL], F32, name="square")
         nc.vector.tensor_tensor(square[:], diff[:], diff[:], ALU.mult)
-        dist2 = held.tile([P, ATOMS], F32, name="dist2")
+        dist2 = held.tile([P, PER_CRYSTAL], F32, name="dist2")
         nc.vector.tensor_reduce(dist2[:], square[:].rearrange("p d n -> p n d"), AXIS.X, ALU.add)
-        rbf = held.tile([P, ATOMS], F32, name="rbf")
+        rbf = held.tile([P, PER_CRYSTAL], F32, name="rbf")
         nc.scalar.activation(rbf[:], dist2[:], ACT.Exp, bias=eps_bias[:], scale=-GAMMA)
 
-        for c in range(CRYSTALS):
-            own = slice(c * PER_CRYSTAL, (c + 1) * PER_CRYSTAL)
-            nc.sync.dma_start(out[0:PER_CRYSTAL, own], rbf[own, own])
+        for own in halves:
+            nc.sync.dma_start(out[0:PER_CRYSTAL, own], rbf[own, :])
 
-        own_rows = held.tile([P, PIECE, CRYSTALS, PER_CRYSTAL], F32, name="own_rows")
-        nc.vector.tensor_tensor(
-            own_rows[:],
-            at_place[:].unsqueeze(3).to_broadcast([P, PIECE, CRYSTALS, PER_CRYSTAL]),
-            rbf[:].rearrange("p (c j) -> p c j", c=CRYSTALS).unsqueeze(1).to_broadcast([P, PIECE, CRYSTALS, PER_CRYSTAL]),
-            ALU.mult,
-        )
-
-        def prepare(batch):
-            if batch == 0:
-                parts = []
-                for g in range(first_pieces):
-                    rbf_piece = spread.tile([P, PIECE * ATOMS], F32, name="rbf_piece")
-                    nc.tensor.matmul(
-                        rbf_piece[:],
-                        pick_piece[:, g, :],
-                        own_rows[:].rearrange("p l c j -> p (l c j)"),
-                        start=True,
-                        stop=True,
-                    )
-                    parts.append(rbf_piece[:])
-            else:
+        def spread_rbf(batch):
+            if batch > 0:
                 rows = slice(batch * BATCH, (batch + 1) * BATCH)
                 rbf_all = batches.tile([P, BATCH * ATOMS], F32, name="rbf_all")
                 nc.sync.dma_start(rbf_all[:], out[rows, :].rearrange("r n -> (r n)").partition_broadcast(P))
-                parts = [rbf_all[:]]
-            v = batches.tile([P, BATCH * ATOMS], F32, name="v")
-            for span, part in spans(parts):
-                nc.vector.tensor_scalar(v[:, span], part, edge_w_sb[:], edge_b_sb[:], ALU.mult, ALU.add)
-            return parts, v
+                return [rbf_all[:]]
+            parts = []
+            for first in range(0, BATCH, PIECE):
+                rbf_piece = spread.tile([P, PIECE * ATOMS], F32, name="rbf_piece")
+                for r in range(PIECE):
+                    column = rbf[:, first + r : first + r + 1]
+                    nc.tensor.transpose(rbf_piece[:, r * ATOMS : (r + 1) * ATOMS], column.to_broadcast([P, P]), identity[:])
+                parts.append(rbf_piece[:])
+            return parts
 
         def spans(parts):
             width = BATCH * ATOMS // len(parts)
             return [(slice(n * width, (n + 1) * width), part) for n, part in enumerate(parts)]
+
+        def make_v(parts):
+            v = batches.tile([P, BATCH * ATOMS], F32, name="v")
+            for span, part in spans(parts):
+                nc.vector.tensor_scalar(v[:, span], part, edge_w_sb[:], edge_b_sb[:], ALU.mult, ALU.add)
+            return v
 
         agg_pairs = held.tile([P, ATOMS], F32, name="agg_pairs")
 
@@ -137,15 +112,16 @@ def tile_crystalencoder_kernel(tc, table, cart, edge_w, edge_b, node_w, node_b, 
             nc.vector.tensor_reduce(agg_pairs[:, done : done + BATCH * CRYSTALS], partial[:], AXIS.X, ALU.add)
 
         n_batches = PER_CRYSTAL // BATCH
-        parts, v = prepare(0)
+        parts = spread_rbf(0)
         for batch in range(n_batches):
             sigmoid = batches.tile([P, BATCH * ATOMS], F32, name="sigmoid")
             for span, part in spans(parts):
                 nc.scalar.activation(sigmoid[:, span], part, ACT.Sigmoid, bias=minus_b[:], scale=minus_w[:])
-            v_now = v
+            v_now = make_v(parts) if batch == 0 else v
             partial = sums.tile([P, BATCH * CRYSTALS, J_LO], F32, name="partial")
             if batch + 1 < n_batches:
-                parts, v = prepare(batch + 1)
+                parts = spread_rbf(batch + 1)
+                v = make_v(parts)
             for first in range(0, BATCH, PIECE):
                 span = slice(first * ATOMS, (first + PIECE) * ATOMS)
                 log_part = pieces.tile([P, PIECE * ATOMS], F32, name="log_part")

@@ -80,30 +80,39 @@ def tile_crystalencoder_kernel(tc, table, cart, edge_w, edge_b, node_w, node_b, 
         for own in halves:
             nc.sync.dma_start(out[0:PER_CRYSTAL, own], rbf[own, :])
 
+        n_batches = PER_CRYSTAL // BATCH
+        gates = [held.tile([P, BATCH, CRYSTALS, PER_CRYSTAL], F32, name=f"gates{b}") for b in range(n_batches)]
+
+        def as_rows(flat, rows):
+            return flat.rearrange("p (r c j) -> p r c j", r=rows, c=CRYSTALS)
+
         def spread_rbf(batch):
             if batch > 0:
                 rows = slice(batch * BATCH, (batch + 1) * BATCH)
                 rbf_all = batches.tile([P, BATCH * ATOMS], F32, name="rbf_all")
                 nc.sync.dma_start(rbf_all[:], out[rows, :].rearrange("r n -> (r n)").partition_broadcast(P))
-                return [rbf_all[:]]
+                return [as_rows(rbf_all[:], BATCH)[:, :, :, batch * BATCH :]]
             parts = []
             for first in range(0, BATCH, PIECE):
                 rbf_piece = spread.tile([P, PIECE * ATOMS], F32, name="rbf_piece")
                 for r in range(PIECE):
                     column = rbf[:, first + r : first + r + 1]
                     nc.tensor.transpose(rbf_piece[:, r * ATOMS : (r + 1) * ATOMS], column.to_broadcast([P, P]), identity[:])
-                parts.append(rbf_piece[:])
+                parts.append(as_rows(rbf_piece[:], PIECE))
             return parts
 
-        def spans(parts):
-            width = BATCH * ATOMS // len(parts)
-            return [(slice(n * width, (n + 1) * width), part) for n, part in enumerate(parts)]
+        def slices_for(parts, tile_of_batch, width):
+            share = width // len(parts)
+            return [as_rows(tile_of_batch[:, n * share : (n + 1) * share], BATCH // len(parts)) for n in range(len(parts))]
 
-        def make_v(parts):
-            v = batches.tile([P, BATCH * ATOMS], F32, name="v")
-            for span, part in spans(parts):
-                nc.vector.tensor_scalar(v[:, span], part, edge_w_sb[:], edge_b_sb[:], ALU.mult, ALU.add)
+        def make_v(parts, width):
+            v = batches.tile([P, width], F32, name="v")
+            for target, part in zip(slices_for(parts, v, width), parts):
+                nc.vector.tensor_scalar(target, part, edge_w_sb[:], edge_b_sb[:], ALU.mult, ALU.add)
             return v
+
+        def computed(batch):
+            return CRYSTALS * (PER_CRYSTAL - batch * BATCH)
 
         agg_pairs = held.tile([P, ATOMS], F32, name="agg_pairs")
 
@@ -111,28 +120,37 @@ def tile_crystalencoder_kernel(tc, table, cart, edge_w, edge_b, node_w, node_b, 
             done = batch * BATCH * CRYSTALS
             nc.vector.tensor_reduce(agg_pairs[:, done : done + BATCH * CRYSTALS], partial[:], AXIS.X, ALU.add)
 
-        n_batches = PER_CRYSTAL // BATCH
         parts = spread_rbf(0)
         for batch in range(n_batches):
-            sigmoid = batches.tile([P, BATCH * ATOMS], F32, name="sigmoid")
-            for span, part in spans(parts):
-                nc.scalar.activation(sigmoid[:, span], part, ACT.Sigmoid, bias=minus_b[:], scale=minus_w[:])
-            v_now = make_v(parts) if batch == 0 else v
+            lo = batch * BATCH
+            cols = computed(batch)
+            sigmoid = batches.tile([P, BATCH * cols], F32, name="sigmoid")
+            for target, part in zip(slices_for(parts, sigmoid, BATCH * cols), parts):
+                nc.scalar.activation(target, part, ACT.Sigmoid, bias=minus_b[:], scale=minus_w[:])
+            v_now = make_v(parts, BATCH * cols) if batch == 0 else v
             partial = sums.tile([P, BATCH * CRYSTALS, J_LO], F32, name="partial")
             if batch + 1 < n_batches:
                 parts = spread_rbf(batch + 1)
-                v = make_v(parts)
+                v = make_v(parts, BATCH * computed(batch + 1))
             for first in range(0, BATCH, PIECE):
-                span = slice(first * ATOMS, (first + PIECE) * ATOMS)
-                log_part = pieces.tile([P, PIECE * ATOMS], F32, name="log_part")
+                span = slice(first * cols, (first + PIECE) * cols)
+                log_part = pieces.tile([P, PIECE * cols], F32, name="log_part")
                 nc.scalar.activation(log_part[:], sigmoid[:, span], ACT.Ln, bias=FLOOR)
-                gate = pieces.tile([P, PIECE * ATOMS], F32, name="gate")
-                nc.vector.scalar_tensor_tensor(gate[:], log_part[:], -1.0, v_now[:, span], ALU.mult, ALU.max)
+                nc.vector.scalar_tensor_tensor(
+                    gates[batch][:, first : first + PIECE, :, lo:],
+                    as_rows(log_part[:], PIECE),
+                    -1.0,
+                    as_rows(v_now[:, span], PIECE),
+                    ALU.mult,
+                    ALU.max,
+                )
                 messages = pieces.tile([P, PIECE * ATOMS], F32, name="messages")
                 for r in range(PIECE):
-                    pair = slice(r * ATOMS, (r + 1) * ATOMS)
                     nc.vector.tensor_tensor(
-                        messages[:, pair], table_sb[:].indirect(offsets[:]), gate[:, pair], ALU.mult
+                        messages[:, r * ATOMS : (r + 1) * ATOMS],
+                        table_sb[:].indirect(offsets[:]),
+                        gates[batch][:, first + r : first + r + 1, :, :].rearrange("p r c j -> p (r c j)"),
+                        ALU.mult,
                     )
                 slices = messages[:].rearrange("p (q h l) -> p q h l", h=J_HI, l=J_LO)
                 sums_of_piece = partial[:, first * CRYSTALS : (first + PIECE) * CRYSTALS, :]
@@ -143,6 +161,11 @@ def tile_crystalencoder_kernel(tc, table, cart, edge_w, edge_b, node_w, node_b, 
                 if first == 0 and batch > 0:
                     add_partial_sums(batch - 1, partial_before)
             partial_before = partial
+            for later in range(batch + 1, n_batches):
+                nc.vector.tensor_copy(
+                    gates[later][:, :, :, lo : lo + BATCH],
+                    gates[batch][:, :, :, later * BATCH : (later + 1) * BATCH].rearrange("p j c r -> p r c j"),
+                )
         add_partial_sums(n_batches - 1, partial_before)
 
         agg_bf = held.tile([P, ATOMS], BF16, name="agg_bf")

@@ -114,11 +114,14 @@ def tile_crystalencoder_kernel(tc, table, cart, edge_w, edge_b, node_w, node_b, 
         def computed(batch):
             return CRYSTALS * (PER_CRYSTAL - batch * BATCH)
 
-        agg_pairs = held.tile([P, ATOMS], F32, name="agg_pairs")
+        agg_pairs = held.tile([P, ATOMS], BF16, name="agg_pairs")
 
-        def add_partial_sums(batch, partial):
-            done = batch * BATCH * CRYSTALS
-            nc.vector.tensor_reduce(agg_pairs[:, done : done + BATCH * CRYSTALS], partial[:], AXIS.X, ALU.add)
+        def add_up(first_pair, terms):
+            atoms = terms.shape[1]
+            with nc.allow_low_precision(reason="agg is rounded to bfloat16 for the matmul with node_w"):
+                nc.vector.tensor_reduce(
+                    agg_pairs[:, first_pair * CRYSTALS : first_pair * CRYSTALS + atoms], terms, AXIS.X, ALU.add
+                )
 
         parts = spread_rbf(0)
         for batch in range(n_batches):
@@ -152,29 +155,33 @@ def tile_crystalencoder_kernel(tc, table, cart, edge_w, edge_b, node_w, node_b, 
                         gates[batch][:, first + r : first + r + 1, :, :].rearrange("p r c j -> p (r c j)"),
                         ALU.mult,
                     )
-                slices = messages[:].rearrange("p (q h l) -> p q h l", h=J_HI, l=J_LO)
-                sums_of_piece = partial[:, first * CRYSTALS : (first + PIECE) * CRYSTALS, :]
-                for h in range(J_HI):
-                    nc.tensor.matmul(
-                        sums_of_piece, identity[:], slices[:, :, h, :], start=(h == 0), stop=(h == J_HI - 1)
-                    )
+                if batch == n_batches - 1 and first == BATCH - PIECE:
+                    add_up(lo, partial[:, 0 : first * CRYSTALS, :])
+                    add_up(lo + first, messages[:].rearrange("p (q j) -> p q j", j=PER_CRYSTAL))
+                else:
+                    slices = messages[:].rearrange("p (q h l) -> p q h l", h=J_HI, l=J_LO)
+                    sums_of_piece = partial[:, first * CRYSTALS : (first + PIECE) * CRYSTALS, :]
+                    for h in range(J_HI):
+                        nc.tensor.matmul(
+                            sums_of_piece, identity[:], slices[:, :, h, :], start=(h == 0), stop=(h == J_HI - 1)
+                        )
                 if first == 0 and batch > 0:
-                    add_partial_sums(batch - 1, partial_before)
+                    add_up(lo - BATCH, partial_before[:])
             partial_before = partial
             for later in range(batch + 1, n_batches):
                 nc.vector.tensor_copy(
                     gates[later][:, :, :, lo : lo + BATCH],
                     gates[batch][:, :, :, later * BATCH : (later + 1) * BATCH].rearrange("p j c r -> p r c j"),
                 )
-        add_partial_sums(n_batches - 1, partial_before)
 
-        agg_bf = held.tile([P, ATOMS], BF16, name="agg_bf")
-        nc.vector.tensor_copy(
-            agg_bf[:].rearrange("p (c r) -> p c r", c=CRYSTALS),
-            agg_pairs[:].rearrange("p (r c) -> p c r", c=CRYSTALS),
-        )
         projected = psum.tile([P, ATOMS], F32, name="projected")
-        nc.tensor.matmul(projected[:], node_w_sb[:], agg_bf[:], start=True, stop=True)
+        nc.tensor.matmul(
+            projected[:].rearrange("p (c r) -> p c r", c=CRYSTALS),
+            node_w_sb[:],
+            agg_pairs[:].rearrange("p (r c) -> p c r", c=CRYSTALS),
+            start=True,
+            stop=True,
+        )
         update = held.tile([P, ATOMS], F32, name="update")
         nc.scalar.activation(update[:], projected[:], ACT.Silu, bias=node_b_sb[:])
         result = held.tile([P, ATOMS], F32, name="result")

@@ -63,6 +63,10 @@ def tile_crystalencoder_kernel(tc, table, cart, edge_w, edge_b, node_w, node_b, 
         nc.vector.tensor_scalar_mul(minus_w[:], edge_w_sb[:], -1.0)
         minus_b = held.tile([P, 1], F32, name="minus_b")
         nc.vector.tensor_scalar_mul(minus_b[:], edge_b_sb[:], -1.0)
+        minus_w_diagonal = held.tile([P, P], F32, name="minus_w_diagonal")
+        nc.gpsimd.tensor_scalar_mul(minus_w_diagonal[:], identity[:], minus_w[:])
+        minus_node_w = held.tile([P, P], BF16, name="minus_node_w")
+        nc.gpsimd.tensor_scalar_mul(minus_node_w[:], node_w_sb[:], -1.0)
 
         eps_bias = held.tile([P, 1], F32, name="eps_bias")
         nc.vector.memset(eps_bias[:], -GAMMA * EPS)
@@ -81,7 +85,9 @@ def tile_crystalencoder_kernel(tc, table, cart, edge_w, edge_b, node_w, node_b, 
             nc.sync.dma_start(out[0:PER_CRYSTAL, own], rbf[own, :])
 
         n_batches = PER_CRYSTAL // BATCH
-        gates = [held.tile([P, BATCH, CRYSTALS, PER_CRYSTAL], F32, name=f"gates{b}") for b in range(n_batches)]
+        minus_gates = [
+            held.tile([P, BATCH, CRYSTALS, PER_CRYSTAL], F32, name=f"minus_gates{b}") for b in range(n_batches)
+        ]
 
         def as_rows(flat, rows):
             return flat.rearrange("p (r c j) -> p r c j", r=rows, c=CRYSTALS)
@@ -105,14 +111,26 @@ def tile_crystalencoder_kernel(tc, table, cart, edge_w, edge_b, node_w, node_b, 
             share = width // len(parts)
             return [as_rows(tile_of_batch[:, n * share : (n + 1) * share], BATCH // len(parts)) for n in range(len(parts))]
 
-        def make_v(parts, width):
-            v = batches.tile([P, width], F32, name="v")
-            for target, part in zip(slices_for(parts, v, width), parts):
-                nc.vector.tensor_scalar(target, part, edge_w_sb[:], edge_b_sb[:], ALU.mult, ALU.add)
-            return v
-
         def computed(batch):
             return CRYSTALS * (PER_CRYSTAL - batch * BATCH)
+
+        def make_minus_wx(batch, parts):
+            width = BATCH * computed(batch)
+            if batch == 0:
+                first_wx = held.tile([P, width], F32, name="first_wx")
+                wx_pieces = slices_for(parts, first_wx, width)
+                for wx_piece, part in zip(wx_pieces, parts):
+                    nc.vector.tensor_scalar_mul(wx_piece, part, minus_w[:])
+                return wx_pieces
+            wx_pieces = []
+            for first in range(0, BATCH, PIECE):
+                wx_bank = spread.tile([P, PIECE * ATOMS], F32, name="wx_bank", tag="rbf_piece")
+                wx_piece = as_rows(wx_bank[:, 0 : width * PIECE // BATCH], PIECE)
+                nc.tensor.matmul(
+                    wx_piece, minus_w_diagonal[:], parts[0][:, first : first + PIECE, :, :], start=True, stop=True
+                )
+                wx_pieces.append(wx_piece)
+            return wx_pieces
 
         agg_pairs = held.tile([P, ATOMS], BF16, name="agg_pairs")
 
@@ -130,29 +148,29 @@ def tile_crystalencoder_kernel(tc, table, cart, edge_w, edge_b, node_w, node_b, 
             sigmoid = batches.tile([P, BATCH * cols], F32, name="sigmoid")
             for target, part in zip(slices_for(parts, sigmoid, BATCH * cols), parts):
                 nc.scalar.activation(target, part, ACT.Sigmoid, bias=minus_b[:], scale=minus_w[:])
-            v_now = make_v(parts, BATCH * cols) if batch == 0 else v
+            wx_now = make_minus_wx(0, parts) if batch == 0 else wx_next
             partial = sums.tile([P, BATCH * CRYSTALS, J_LO], F32, name="partial")
             if batch + 1 < n_batches:
                 parts = spread_rbf(batch + 1)
-                v = make_v(parts, BATCH * computed(batch + 1))
+                wx_next = make_minus_wx(batch + 1, parts)
             for first in range(0, BATCH, PIECE):
                 span = slice(first * cols, (first + PIECE) * cols)
                 log_part = pieces.tile([P, PIECE * cols], F32, name="log_part")
                 nc.scalar.activation(log_part[:], sigmoid[:, span], ACT.Ln, bias=FLOOR)
                 nc.vector.scalar_tensor_tensor(
-                    gates[batch][:, first : first + PIECE, :, lo:],
+                    minus_gates[batch][:, first : first + PIECE, :, lo:],
+                    wx_now[first // PIECE],
+                    minus_b[:],
                     as_rows(log_part[:], PIECE),
-                    -1.0,
-                    as_rows(v_now[:, span], PIECE),
-                    ALU.mult,
-                    ALU.max,
+                    ALU.add,
+                    ALU.min,
                 )
                 messages = pieces.tile([P, PIECE * ATOMS], F32, name="messages")
                 for r in range(PIECE):
                     nc.vector.tensor_tensor(
                         messages[:, r * ATOMS : (r + 1) * ATOMS],
                         table_sb[:].indirect(offsets[:]),
-                        gates[batch][:, first + r : first + r + 1, :, :].rearrange("p r c j -> p (r c j)"),
+                        minus_gates[batch][:, first + r : first + r + 1, :, :].rearrange("p r c j -> p (r c j)"),
                         ALU.mult,
                     )
                 if batch == n_batches - 1 and first == BATCH - PIECE:
@@ -170,14 +188,14 @@ def tile_crystalencoder_kernel(tc, table, cart, edge_w, edge_b, node_w, node_b, 
             partial_before = partial
             for later in range(batch + 1, n_batches):
                 nc.vector.tensor_copy(
-                    gates[later][:, :, :, lo : lo + BATCH],
-                    gates[batch][:, :, :, later * BATCH : (later + 1) * BATCH].rearrange("p j c r -> p r c j"),
+                    minus_gates[later][:, :, :, lo : lo + BATCH],
+                    minus_gates[batch][:, :, :, later * BATCH : (later + 1) * BATCH].rearrange("p j c r -> p r c j"),
                 )
 
         projected = psum.tile([P, ATOMS], F32, name="projected")
         nc.tensor.matmul(
             projected[:].rearrange("p (c r) -> p c r", c=CRYSTALS),
-            node_w_sb[:],
+            minus_node_w[:],
             agg_pairs[:].rearrange("p (r c) -> p c r", c=CRYSTALS),
             start=True,
             stop=True,

@@ -18,8 +18,10 @@ GAMMA = 1.0 / 64.0
 EPS = 1e-6
 BATCH = 16
 PIECE = 4
-J_HI = 4
+J_HI = 8
 J_LO = PER_CRYSTAL // J_HI
+FOLD = 8
+BANK = 512
 FLOOR = 2.0**-60
 
 FLOPS = 2 * P * P * ATOMS
@@ -31,6 +33,7 @@ def tile_crystalencoder_kernel(tc, table, cart, edge_w, edge_b, node_w, node_b, 
         tc.tile_pool(name="held", bufs=1) as held,
         tc.tile_pool(name="batches", bufs=2) as batches,
         tc.tile_pool(name="pieces", bufs=4) as pieces,
+        tc.tile_pool(name="folds", bufs=3) as folds,
         tc.psum_pool(name="psum", bufs=1) as psum,
         tc.psum_pool(name="sums", bufs=2) as sums,
         tc.psum_pool(name="spread", bufs=BATCH // PIECE) as spread,
@@ -149,7 +152,8 @@ def tile_crystalencoder_kernel(tc, table, cart, edge_w, edge_b, node_w, node_b, 
             for target, part in zip(slices_for(parts, sigmoid, BATCH * cols), parts):
                 nc.scalar.activation(target, part, ACT.Sigmoid, bias=minus_b[:], scale=minus_w[:])
             wx_now = make_minus_wx(0, parts) if batch == 0 else wx_next
-            partial = sums.tile([P, BATCH * CRYSTALS, J_LO], F32, name="partial")
+            bank = sums.tile([P, BANK], F32, name="bank")
+            partial = bank[:, 0 : BATCH * CRYSTALS * J_LO].rearrange("p (q l) -> p q l", l=J_LO)
             if batch + 1 < n_batches:
                 parts = spread_rbf(batch + 1)
                 wx_next = make_minus_wx(batch + 1, parts)
@@ -165,26 +169,29 @@ def tile_crystalencoder_kernel(tc, table, cart, edge_w, edge_b, node_w, node_b, 
                     ALU.add,
                     ALU.min,
                 )
-                messages = pieces.tile([P, PIECE * ATOMS], F32, name="messages")
+                if first % FOLD == 0:
+                    messages = folds.tile([P, FOLD * ATOMS], F32, name="messages")
                 for r in range(PIECE):
+                    place = first % FOLD + r
                     nc.vector.tensor_tensor(
-                        messages[:, r * ATOMS : (r + 1) * ATOMS],
+                        messages[:, place * ATOMS : (place + 1) * ATOMS],
                         table_sb[:].indirect(offsets[:]),
                         minus_gates[batch][:, first + r : first + r + 1, :, :].rearrange("p r c j -> p (r c j)"),
                         ALU.mult,
                     )
-                if batch == n_batches - 1 and first == BATCH - PIECE:
-                    add_up(lo, partial[:, 0 : first * CRYSTALS, :])
-                    add_up(lo + first, messages[:].rearrange("p (q j) -> p q j", j=PER_CRYSTAL))
-                else:
+                group = first + PIECE - FOLD
+                if group % FOLD == 0 and batch == n_batches - 1 and group == BATCH - FOLD:
+                    add_up(lo, partial[:, 0 : group * CRYSTALS, :])
+                    add_up(lo + group, messages[:].rearrange("p (q j) -> p q j", j=PER_CRYSTAL))
+                elif group % FOLD == 0:
                     slices = messages[:].rearrange("p (q h l) -> p q h l", h=J_HI, l=J_LO)
-                    sums_of_piece = partial[:, first * CRYSTALS : (first + PIECE) * CRYSTALS, :]
+                    sums_of_group = partial[:, group * CRYSTALS : (group + FOLD) * CRYSTALS, :]
                     for h in range(J_HI):
                         nc.tensor.matmul(
-                            sums_of_piece, identity[:], slices[:, :, h, :], start=(h == 0), stop=(h == J_HI - 1)
+                            sums_of_group, identity[:], slices[:, :, h, :], start=(h == 0), stop=(h == J_HI - 1)
                         )
-                if first == 0 and batch > 0:
-                    add_up(lo - BATCH, partial_before[:])
+                if first == PIECE and batch > 0:
+                    add_up(lo - BATCH, partial_before)
             partial_before = partial
             for later in range(batch + 1, n_batches):
                 nc.vector.tensor_copy(

@@ -13,15 +13,13 @@ TYPES = 256
 ATOMS = 128
 CRYSTALS = 2
 PER_CRYSTAL = ATOMS // CRYSTALS
+HALF = PER_CRYSTAL // 2
 DIMS = 3
 GAMMA = 1.0 / 64.0
 EPS = 1e-6
-BATCH = 16
+SHIFTS = HALF + 1
 PIECE = 4
-J_HI = 8
-J_LO = PER_CRYSTAL // J_HI
-FOLD = 8
-BANK = 512
+BATCH = 2
 FLOOR = 2.0**-60
 
 FLOPS = 2 * P * P * ATOMS
@@ -32,12 +30,13 @@ def tile_crystalencoder_kernel(tc, table, cart, edge_w, edge_b, node_w, node_b, 
     with (
         tc.tile_pool(name="held", bufs=1) as held,
         tc.tile_pool(name="batches", bufs=2) as batches,
-        tc.tile_pool(name="pieces", bufs=4) as pieces,
-        tc.tile_pool(name="folds", bufs=3) as folds,
+        tc.tile_pool(name="logs", bufs=4) as logs,
+        tc.tile_pool(name="ring", bufs=8) as ring,
         tc.psum_pool(name="psum", bufs=1) as psum,
-        tc.psum_pool(name="sums", bufs=2) as sums,
-        tc.psum_pool(name="spread", bufs=BATCH // PIECE) as spread,
+        tc.psum_pool(name="banks", bufs=4) as banks,
     ):
+        identity = held.tile([P, P], F32, name="identity")
+        make_identity(nc, identity[:])
         halves = [slice(c * PER_CRYSTAL, (c + 1) * PER_CRYSTAL) for c in range(CRYSTALS)]
         cart_crystal = held.tile([P, DIMS, PER_CRYSTAL], F32, name="cart_crystal")
         for own, queue in zip(halves, (nc.sync, nc.scalar)):
@@ -47,8 +46,8 @@ def tile_crystalencoder_kernel(tc, table, cart, edge_w, edge_b, node_w, node_b, 
         cart_own = held.tile([P, DIMS], F32, name="cart_own")
         with nc.allow_non_contiguous_dma(reason="three coordinates to a partition"):
             nc.sync.dma_start(cart_own[:], cart.rearrange("d n -> n d"))
-        edge_w_sb = held.tile([P, 1], F32, name="edge_w_sb")
-        nc.sync.dma_start(edge_w_sb[:], edge_w)
+        w_rows = held.tile([P, P], F32, name="w_rows")
+        nc.sync.dma_start(w_rows[:], edge_w.rearrange("c o -> (c o)").partition_broadcast(P))
         edge_b_sb = held.tile([P, 1], F32, name="edge_b_sb")
         nc.scalar.dma_start(edge_b_sb[:], edge_b)
         offsets = held.tile([P, ATOMS // 16], U16, name="offsets")
@@ -60,19 +59,24 @@ def tile_crystalencoder_kernel(tc, table, cart, edge_w, edge_b, node_w, node_b, 
         node_b_sb = held.tile([P, 1], F32, name="node_b_sb")
         nc.gpsimd.dma_start(node_b_sb[:], node_b)
 
-        identity = held.tile([P, P], F32, name="identity")
-        make_identity(nc, identity[:])
-        minus_w = held.tile([P, 1], F32, name="minus_w")
-        nc.vector.tensor_scalar_mul(minus_w[:], edge_w_sb[:], -1.0)
+        shift_mask = held.tile([P, CRYSTALS, PER_CRYSTAL + HALF], F32, name="shift_mask")
+        identity_by_crystal = identity[:].rearrange("p (c n) -> p c n", c=CRYSTALS)
+        nc.vector.tensor_copy(shift_mask[:, :, 0:PER_CRYSTAL], identity_by_crystal)
+        nc.vector.tensor_copy(shift_mask[:, :, PER_CRYSTAL:], identity_by_crystal[:, :, 0:HALF])
+        zeros = held.tile([P, CRYSTALS * ATOMS], F32, name="zeros")
+        nc.vector.memset(zeros[:], 0.0)
+        eps_bias = held.tile([P, 1], F32, name="eps_bias")
+        nc.vector.memset(eps_bias[:], -GAMMA * EPS)
         minus_b = held.tile([P, 1], F32, name="minus_b")
         nc.vector.tensor_scalar_mul(minus_b[:], edge_b_sb[:], -1.0)
-        minus_w_diagonal = held.tile([P, P], F32, name="minus_w_diagonal")
-        nc.gpsimd.tensor_scalar_mul(minus_w_diagonal[:], identity[:], minus_w[:])
+        minus_w_rows = held.tile([P, P], F32, name="minus_w_rows")
+        nc.gpsimd.tensor_scalar_mul(minus_w_rows[:], w_rows[:], -1.0)
         minus_node_w = held.tile([P, P], BF16, name="minus_node_w")
         nc.gpsimd.tensor_scalar_mul(minus_node_w[:], node_w_sb[:], -1.0)
 
-        eps_bias = held.tile([P, 1], F32, name="eps_bias")
-        nc.vector.memset(eps_bias[:], -GAMMA * EPS)
+        sums = psum.tile([P, CRYSTALS, ATOMS], F32, name="sums")
+        nc.tensor.matmul(sums[:].rearrange("p c n -> p (c n)"), identity[:], zeros[:], start=True, stop=False)
+
         diff = held.tile([P, DIMS, PER_CRYSTAL], F32, name="diff")
         nc.vector.tensor_tensor(
             diff[:], cart_crystal[:], cart_own[:].unsqueeze(2).to_broadcast([P, DIMS, PER_CRYSTAL]), ALU.subtract
@@ -84,129 +88,91 @@ def tile_crystalencoder_kernel(tc, table, cart, edge_w, edge_b, node_w, node_b, 
         rbf = held.tile([P, PER_CRYSTAL], F32, name="rbf")
         nc.scalar.activation(rbf[:], dist2[:], ACT.Exp, bias=eps_bias[:], scale=-GAMMA)
 
-        for own in halves:
-            nc.sync.dma_start(out[0:PER_CRYSTAL, own], rbf[own, :])
+        pieces = [range(first, min(first + PIECE, SHIFTS)) for first in range(0, SHIFTS, PIECE)]
+        rbf_both = rbf[:].unsqueeze(1).to_broadcast([P, CRYSTALS, PER_CRYSTAL])
+        picked = []
+        for n, shifts in enumerate(pieces):
+            picked.append(held.tile([P, len(shifts), CRYSTALS, PER_CRYSTAL], F32, name=f"picked{n}"))
+            for r, t in enumerate(shifts):
+                nc.vector.tensor_tensor(picked[n][:, r, :, :], rbf_both, shift_mask[:, :, t : t + PER_CRYSTAL], ALU.mult)
 
-        n_batches = PER_CRYSTAL // BATCH
+        def make_minus_wx(n):
+            bank = banks.tile([P, PIECE * ATOMS], F32, name="bank")
+            minus_wx = bank[:, 0 : len(pieces[n]) * ATOMS]
+            nc.tensor.matmul(
+                minus_wx, minus_w_rows[:], picked[n][:].rearrange("p r c j -> p (r c j)"), start=True, stop=True
+            )
+            return minus_wx
+
+
         minus_gates = [
-            held.tile([P, BATCH, CRYSTALS, PER_CRYSTAL], F32, name=f"minus_gates{b}") for b in range(n_batches)
+            held.tile([P, len(shifts), CRYSTALS, HALF + PER_CRYSTAL], F32, name=f"minus_gates{n}")
+            for n, shifts in enumerate(pieces)
         ]
 
-        def as_rows(flat, rows):
-            return flat.rearrange("p (r c j) -> p r c j", r=rows, c=CRYSTALS)
+        per_crystal_columns = PER_CRYSTAL // 16
 
-        def spread_rbf(batch):
-            if batch > 0:
-                rows = slice(batch * BATCH, (batch + 1) * BATCH)
-                rbf_all = batches.tile([P, BATCH * ATOMS], F32, name="rbf_all")
-                nc.sync.dma_start(rbf_all[:], out[rows, :].rearrange("r n -> (r n)").partition_broadcast(P))
-                return [as_rows(rbf_all[:], BATCH)[:, :, :, batch * BATCH :]]
-            parts = []
-            for first in range(0, BATCH, PIECE):
-                rbf_piece = spread.tile([P, PIECE * ATOMS], F32, name="rbf_piece")
-                for r in range(PIECE):
-                    column = rbf[:, first + r : first + r + 1]
-                    nc.tensor.transpose(rbf_piece[:, r * ATOMS : (r + 1) * ATOMS], column.to_broadcast([P, P]), identity[:])
-                parts.append(as_rows(rbf_piece[:], PIECE))
-            return parts
-
-        def slices_for(parts, tile_of_batch, width):
-            share = width // len(parts)
-            return [as_rows(tile_of_batch[:, n * share : (n + 1) * share], BATCH // len(parts)) for n in range(len(parts))]
-
-        def computed(batch):
-            return CRYSTALS * (PER_CRYSTAL - batch * BATCH)
-
-        def make_minus_wx(batch, parts):
-            width = BATCH * computed(batch)
-            if batch == 0:
-                first_wx = held.tile([P, width], F32, name="first_wx")
-                wx_pieces = slices_for(parts, first_wx, width)
-                for wx_piece, part in zip(wx_pieces, parts):
-                    nc.vector.tensor_scalar_mul(wx_piece, part, minus_w[:])
-                return wx_pieces
-            wx_pieces = []
-            for first in range(0, BATCH, PIECE):
-                wx_bank = spread.tile([P, PIECE * ATOMS], F32, name="wx_bank", tag="rbf_piece")
-                wx_piece = as_rows(wx_bank[:, 0 : width * PIECE // BATCH], PIECE)
-                nc.tensor.matmul(
-                    wx_piece, minus_w_diagonal[:], parts[0][:, first : first + PIECE, :, :], start=True, stop=True
+        def send_messages(n, r, first, shift, last):
+            messages = ring.tile([P, CRYSTALS, PER_CRYSTAL], F32, name="messages")
+            for c in range(CRYSTALS):
+                nc.vector.tensor_tensor(
+                    messages[:, c, :],
+                    table_sb[:].indirect(offsets[:, c * per_crystal_columns : (c + 1) * per_crystal_columns]),
+                    minus_gates[n][:, r, c, first : first + PER_CRYSTAL],
+                    ALU.mult,
                 )
-                wx_pieces.append(wx_piece)
-            return wx_pieces
+            nc.tensor.matmul(sums[:, :, shift : shift + PER_CRYSTAL], identity[:], messages[:], start=False, stop=last)
 
-        agg_pairs = held.tile([P, ATOMS], BF16, name="agg_pairs")
+        def send_piece(n):
+            for r, t in enumerate(pieces[n]):
+                send_messages(n, r, HALF, t, t == SHIFTS - 1)
+            for r, t in enumerate(pieces[n]):
+                if 0 < t < HALF:
+                    send_messages(n, r, HALF - t, PER_CRYSTAL - t, False)
 
-        def add_up(first_pair, terms):
-            atoms = terms.shape[1]
-            with nc.allow_low_precision(reason="agg is rounded to bfloat16 for the matmul with node_w"):
-                nc.vector.tensor_reduce(
-                    agg_pairs[:, first_pair * CRYSTALS : first_pair * CRYSTALS + atoms], terms, AXIS.X, ALU.add
-                )
+        n_batches = len(pieces) // BATCH
+        batch_pieces = [list(range(b * BATCH, (b + 1) * BATCH)) for b in range(n_batches)]
+        batch_pieces[-1].extend(range(n_batches * BATCH, len(pieces)))
 
-        parts = spread_rbf(0)
-        for batch in range(n_batches):
-            lo = batch * BATCH
-            cols = computed(batch)
-            sigmoid = batches.tile([P, BATCH * cols], F32, name="sigmoid")
-            for target, part in zip(slices_for(parts, sigmoid, BATCH * cols), parts):
-                nc.scalar.activation(target, part, ACT.Sigmoid, bias=minus_b[:], scale=minus_w[:])
-            wx_now = make_minus_wx(0, parts) if batch == 0 else wx_next
-            bank = sums.tile([P, BANK], F32, name="bank")
-            partial = bank[:, 0 : BATCH * CRYSTALS * J_LO].rearrange("p (q l) -> p q l", l=J_LO)
-            if batch + 1 < n_batches:
-                parts = spread_rbf(batch + 1)
-                wx_next = make_minus_wx(batch + 1, parts)
-            for first in range(0, BATCH, PIECE):
-                span = slice(first * cols, (first + PIECE) * cols)
-                log_part = pieces.tile([P, PIECE * cols], F32, name="log_part")
-                nc.scalar.activation(log_part[:], sigmoid[:, span], ACT.Ln, bias=FLOOR)
+        minus_wx = {n: make_minus_wx(n) for n in batch_pieces[0]}
+        made = None
+        for b, members in enumerate(batch_pieces):
+            sigmoid = batches.tile([P, (BATCH + 1) * PIECE * ATOMS], F32, name="sigmoid")
+            spans = {}
+            for place, n in enumerate(members):
+                spans[n] = slice(place * PIECE * ATOMS, place * PIECE * ATOMS + len(pieces[n]) * ATOMS)
+                nc.scalar.activation(sigmoid[:, spans[n]], minus_wx[n], ACT.Sigmoid, bias=minus_b[:])
+            if b + 1 < n_batches:
+                for n in batch_pieces[b + 1]:
+                    minus_wx[n] = make_minus_wx(n)
+            for n in members:
+                width = len(pieces[n]) * ATOMS
+                log_part = logs.tile([P, PIECE * ATOMS], F32, name="log_part")
+                nc.scalar.activation(log_part[:, 0:width], sigmoid[:, spans[n]], ACT.Ln, bias=FLOOR)
                 nc.vector.scalar_tensor_tensor(
-                    minus_gates[batch][:, first : first + PIECE, :, lo:],
-                    wx_now[first // PIECE],
+                    minus_gates[n][:, :, :, HALF:],
+                    minus_wx[n].rearrange("p (r c j) -> p r c j", c=CRYSTALS, j=PER_CRYSTAL),
                     minus_b[:],
-                    as_rows(log_part[:], PIECE),
+                    log_part[:, 0:width].rearrange("p (r c j) -> p r c j", c=CRYSTALS, j=PER_CRYSTAL),
                     ALU.add,
                     ALU.min,
                 )
-                if first % FOLD == 0:
-                    messages = folds.tile([P, FOLD * ATOMS], F32, name="messages")
-                for r in range(PIECE):
-                    place = first % FOLD + r
-                    nc.vector.tensor_tensor(
-                        messages[:, place * ATOMS : (place + 1) * ATOMS],
-                        table_sb[:].indirect(offsets[:]),
-                        minus_gates[batch][:, first + r : first + r + 1, :, :].rearrange("p r c j -> p (r c j)"),
-                        ALU.mult,
+                reach = max([t for t in pieces[n] if t < HALF] + [0])
+                if reach > 0:
+                    nc.scalar.copy(
+                        minus_gates[n][:, :, :, HALF - reach : HALF],
+                        minus_gates[n][:, :, :, HALF + PER_CRYSTAL - reach :],
                     )
-                group = first + PIECE - FOLD
-                if group % FOLD == 0 and batch == n_batches - 1 and group == BATCH - FOLD:
-                    add_up(lo, partial[:, 0 : group * CRYSTALS, :])
-                    add_up(lo + group, messages[:].rearrange("p (q j) -> p q j", j=PER_CRYSTAL))
-                elif group % FOLD == 0:
-                    slices = messages[:].rearrange("p (q h l) -> p q h l", h=J_HI, l=J_LO)
-                    sums_of_group = partial[:, group * CRYSTALS : (group + FOLD) * CRYSTALS, :]
-                    for h in range(J_HI):
-                        nc.tensor.matmul(
-                            sums_of_group, identity[:], slices[:, :, h, :], start=(h == 0), stop=(h == J_HI - 1)
-                        )
-                if first == PIECE and batch > 0:
-                    add_up(lo - BATCH, partial_before)
-            partial_before = partial
-            for later in range(batch + 1, n_batches):
-                nc.vector.tensor_copy(
-                    minus_gates[later][:, :, :, lo : lo + BATCH],
-                    minus_gates[batch][:, :, :, later * BATCH : (later + 1) * BATCH].rearrange("p j c r -> p r c j"),
-                )
+                if made is not None:
+                    send_piece(made)
+                made = n
+        send_piece(made)
 
+        agg = held.tile([P, CRYSTALS, PER_CRYSTAL], BF16, name="agg")
+        with nc.allow_low_precision(reason="agg is rounded to bfloat16 for the matmul with node_w"):
+            nc.vector.tensor_reduce(agg[:], sums[:].rearrange("p c (h i) -> p c i h", h=2), AXIS.X, ALU.add)
         projected = psum.tile([P, ATOMS], F32, name="projected")
-        nc.tensor.matmul(
-            projected[:].rearrange("p (c r) -> p c r", c=CRYSTALS),
-            minus_node_w[:],
-            agg_pairs[:].rearrange("p (r c) -> p c r", c=CRYSTALS),
-            start=True,
-            stop=True,
-        )
+        nc.tensor.matmul(projected[:], minus_node_w[:], agg[:].rearrange("p c i -> p (c i)"), start=True, stop=True)
         update = held.tile([P, ATOMS], F32, name="update")
         nc.scalar.activation(update[:], projected[:], ACT.Silu, bias=node_b_sb[:])
         result = held.tile([P, ATOMS], F32, name="result")

@@ -17,9 +17,10 @@ HALF = PER_CRYSTAL // 2
 DIMS = 3
 GAMMA = 1.0 / 64.0
 EPS = 1e-6
-SHIFTS = HALF + 1
+STEPS = HALF + 1
 PIECE = 4
 BATCH = 2
+BANK = 512
 FLOOR = 2.0**-60
 
 FLOPS = 2 * P * P * ATOMS
@@ -59,10 +60,10 @@ def tile_crystalencoder_kernel(tc, table, cart, edge_w, edge_b, node_w, node_b, 
         node_b_sb = held.tile([P, 1], F32, name="node_b_sb")
         nc.gpsimd.dma_start(node_b_sb[:], node_b)
 
-        shift_mask = held.tile([P, CRYSTALS, PER_CRYSTAL + HALF], F32, name="shift_mask")
+        shift_mask = held.tile([P, CRYSTALS, 2 * PER_CRYSTAL], F32, name="shift_mask")
         identity_by_crystal = identity[:].rearrange("p (c n) -> p c n", c=CRYSTALS)
         nc.vector.tensor_copy(shift_mask[:, :, 0:PER_CRYSTAL], identity_by_crystal)
-        nc.vector.tensor_copy(shift_mask[:, :, PER_CRYSTAL:], identity_by_crystal[:, :, 0:HALF])
+        nc.vector.tensor_copy(shift_mask[:, :, PER_CRYSTAL:], identity_by_crystal)
         zeros = held.tile([P, CRYSTALS * ATOMS], F32, name="zeros")
         nc.vector.memset(zeros[:], 0.0)
         eps_bias = held.tile([P, 1], F32, name="eps_bias")
@@ -74,8 +75,12 @@ def tile_crystalencoder_kernel(tc, table, cart, edge_w, edge_b, node_w, node_b, 
         minus_node_w = held.tile([P, P], BF16, name="minus_node_w")
         nc.gpsimd.tensor_scalar_mul(minus_node_w[:], node_w_sb[:], -1.0)
 
-        sums = psum.tile([P, CRYSTALS, ATOMS], F32, name="sums")
-        nc.tensor.matmul(sums[:].rearrange("p c n -> p (c n)"), identity[:], zeros[:], start=True, stop=False)
+        sums = psum.tile([P, BANK], F32, name="sums")
+        nc.tensor.matmul(sums[:, 0 : CRYSTALS * ATOMS], identity[:], zeros[:], start=True, stop=False)
+
+        def sums_from(s0, s1):
+            apart = ATOMS + s1 - s0
+            return sums[:, s0 : s0 + CRYSTALS * apart].rearrange("p (c n) -> p c n", c=CRYSTALS)[:, :, 0:PER_CRYSTAL]
 
         diff = held.tile([P, DIMS, PER_CRYSTAL], F32, name="diff")
         nc.vector.tensor_tensor(
@@ -88,13 +93,13 @@ def tile_crystalencoder_kernel(tc, table, cart, edge_w, edge_b, node_w, node_b, 
         rbf = held.tile([P, PER_CRYSTAL], F32, name="rbf")
         nc.scalar.activation(rbf[:], dist2[:], ACT.Exp, bias=eps_bias[:], scale=-GAMMA)
 
-        pieces = [range(first, min(first + PIECE, SHIFTS)) for first in range(0, SHIFTS, PIECE)]
-        rbf_both = rbf[:].unsqueeze(1).to_broadcast([P, CRYSTALS, PER_CRYSTAL])
+        pieces = [range(first, min(first + PIECE, STEPS)) for first in range(0, STEPS, PIECE)]
         picked = []
-        for n, shifts in enumerate(pieces):
-            picked.append(held.tile([P, len(shifts), CRYSTALS, PER_CRYSTAL], F32, name=f"picked{n}"))
-            for r, t in enumerate(shifts):
-                nc.vector.tensor_tensor(picked[n][:, r, :, :], rbf_both, shift_mask[:, :, t : t + PER_CRYSTAL], ALU.mult)
+        for n, steps in enumerate(pieces):
+            picked.append(held.tile([P, len(steps), CRYSTALS, PER_CRYSTAL], F32, name=f"picked{n}"))
+            for r, t in enumerate(steps):
+                for c, s in enumerate((t, PER_CRYSTAL - t)):
+                    nc.vector.tensor_tensor(picked[n][:, r, c, :], rbf[:], shift_mask[:, c, s : s + PER_CRYSTAL], ALU.mult)
 
         def make_minus_wx(n):
             bank = banks.tile([P, PIECE * ATOMS], F32, name="bank")
@@ -105,30 +110,35 @@ def tile_crystalencoder_kernel(tc, table, cart, edge_w, edge_b, node_w, node_b, 
             return minus_wx
 
 
+        FIRST = (HALF, HALF + PER_CRYSTAL)
         minus_gates = [
-            held.tile([P, len(shifts), CRYSTALS, HALF + PER_CRYSTAL], F32, name=f"minus_gates{n}")
-            for n, shifts in enumerate(pieces)
+            held.tile([P, len(steps), HALF + ATOMS + HALF], F32, name=f"minus_gates{n}") for n, steps in enumerate(pieces)
         ]
-
         per_crystal_columns = PER_CRYSTAL // 16
-
-        def send_messages(n, r, first, shift, last):
-            messages = ring.tile([P, CRYSTALS, PER_CRYSTAL], F32, name="messages")
-            for c in range(CRYSTALS):
-                nc.vector.tensor_tensor(
-                    messages[:, c, :],
-                    table_sb[:].indirect(offsets[:, c * per_crystal_columns : (c + 1) * per_crystal_columns]),
-                    minus_gates[n][:, r, c, first : first + PER_CRYSTAL],
-                    ALU.mult,
-                )
-            nc.tensor.matmul(sums[:, :, shift : shift + PER_CRYSTAL], identity[:], messages[:], start=False, stop=last)
 
         def send_piece(n):
             for r, t in enumerate(pieces[n]):
-                send_messages(n, r, HALF, t, t == SHIFTS - 1)
+                messages = ring.tile([P, CRYSTALS, PER_CRYSTAL], F32, name="messages")
+                nc.vector.tensor_tensor(
+                    messages[:].rearrange("p c j -> p (c j)"),
+                    table_sb[:].indirect(offsets[:]),
+                    minus_gates[n][:, r, HALF : HALF + ATOMS],
+                    ALU.mult,
+                )
+                nc.tensor.matmul(
+                    sums_from(t, PER_CRYSTAL - t), identity[:], messages[:], start=False, stop=(t == STEPS - 1)
+                )
             for r, t in enumerate(pieces[n]):
                 if 0 < t < HALF:
-                    send_messages(n, r, HALF - t, PER_CRYSTAL - t, False)
+                    messages = ring.tile([P, CRYSTALS, PER_CRYSTAL], F32, name="messages")
+                    for c, first in enumerate((FIRST[0] - t, FIRST[1] + t)):
+                        nc.vector.tensor_tensor(
+                            messages[:, c, :],
+                            table_sb[:].indirect(offsets[:, c * per_crystal_columns : (c + 1) * per_crystal_columns]),
+                            minus_gates[n][:, r, first : first + PER_CRYSTAL],
+                            ALU.mult,
+                        )
+                    nc.tensor.matmul(sums_from(PER_CRYSTAL - t, t), identity[:], messages[:], start=False, stop=False)
 
         n_batches = len(pieces) // BATCH
         batch_pieces = [list(range(b * BATCH, (b + 1) * BATCH)) for b in range(n_batches)]
@@ -150,18 +160,21 @@ def tile_crystalencoder_kernel(tc, table, cart, edge_w, edge_b, node_w, node_b, 
                 log_part = logs.tile([P, PIECE * ATOMS], F32, name="log_part")
                 nc.scalar.activation(log_part[:, 0:width], sigmoid[:, spans[n]], ACT.Ln, bias=FLOOR)
                 nc.vector.scalar_tensor_tensor(
-                    minus_gates[n][:, :, :, HALF:],
-                    minus_wx[n].rearrange("p (r c j) -> p r c j", c=CRYSTALS, j=PER_CRYSTAL),
+                    minus_gates[n][:, :, HALF : HALF + ATOMS],
+                    minus_wx[n].rearrange("p (r a) -> p r a", a=ATOMS),
                     minus_b[:],
-                    log_part[:, 0:width].rearrange("p (r c j) -> p r c j", c=CRYSTALS, j=PER_CRYSTAL),
+                    log_part[:, 0:width].rearrange("p (r a) -> p r a", a=ATOMS),
                     ALU.add,
                     ALU.min,
                 )
                 reach = max([t for t in pieces[n] if t < HALF] + [0])
                 if reach > 0:
                     nc.scalar.copy(
-                        minus_gates[n][:, :, :, HALF - reach : HALF],
-                        minus_gates[n][:, :, :, HALF + PER_CRYSTAL - reach :],
+                        minus_gates[n][:, :, FIRST[0] - reach : FIRST[0]], minus_gates[n][:, :, FIRST[1] - reach : FIRST[1]]
+                    )
+                    nc.scalar.copy(
+                        minus_gates[n][:, :, FIRST[1] + PER_CRYSTAL : FIRST[1] + PER_CRYSTAL + reach],
+                        minus_gates[n][:, :, FIRST[1] : FIRST[1] + reach],
                     )
                 if made is not None:
                     send_piece(made)
@@ -170,7 +183,9 @@ def tile_crystalencoder_kernel(tc, table, cart, edge_w, edge_b, node_w, node_b, 
 
         agg = held.tile([P, CRYSTALS, PER_CRYSTAL], BF16, name="agg")
         with nc.allow_low_precision(reason="agg is rounded to bfloat16 for the matmul with node_w"):
-            nc.vector.tensor_reduce(agg[:], sums[:].rearrange("p c (h i) -> p c i h", h=2), AXIS.X, ALU.add)
+            nc.vector.tensor_reduce(
+                agg[:], sums[:, 0 : CRYSTALS * ATOMS].rearrange("p (c h i) -> p c i h", c=CRYSTALS, h=2), AXIS.X, ALU.add
+            )
         projected = psum.tile([P, ATOMS], F32, name="projected")
         nc.tensor.matmul(projected[:], minus_node_w[:], agg[:].rearrange("p c i -> p (c i)"), start=True, stop=True)
         update = held.tile([P, ATOMS], F32, name="update")

@@ -116,7 +116,13 @@ def tile_crystalencoder_kernel(tc, table, cart, edge_w, edge_b, node_w, node_b, 
         ]
         per_crystal_columns = PER_CRYSTAL // 16
 
-        def send_piece(n):
+        sent = []
+
+        def add_to_sums(messages, s0, s1):
+            sent.append((s0, s1))
+            nc.tensor.matmul(sums_from(s0, s1), identity[:], messages[:], start=False, stop=(len(sent) == PER_CRYSTAL))
+
+        def send_computed(n):
             for r, t in enumerate(pieces[n]):
                 messages = ring.tile([P, CRYSTALS, PER_CRYSTAL], F32, name="messages")
                 nc.vector.tensor_tensor(
@@ -125,9 +131,20 @@ def tile_crystalencoder_kernel(tc, table, cart, edge_w, edge_b, node_w, node_b, 
                     minus_gates[n][:, r, HALF : HALF + ATOMS],
                     ALU.mult,
                 )
-                nc.tensor.matmul(
-                    sums_from(t, PER_CRYSTAL - t), identity[:], messages[:], start=False, stop=(t == STEPS - 1)
+                add_to_sums(messages, t, PER_CRYSTAL - t)
+
+        def repeat_ends(n):
+            reach = max([t for t in pieces[n] if t < HALF] + [0])
+            if reach > 0:
+                nc.scalar.copy(
+                    minus_gates[n][:, :, FIRST[0] - reach : FIRST[0]], minus_gates[n][:, :, FIRST[1] - reach : FIRST[1]]
                 )
+                nc.scalar.copy(
+                    minus_gates[n][:, :, FIRST[1] + PER_CRYSTAL : FIRST[1] + PER_CRYSTAL + reach],
+                    minus_gates[n][:, :, FIRST[1] : FIRST[1] + reach],
+                )
+
+        def send_turned(n):
             for r, t in enumerate(pieces[n]):
                 if 0 < t < HALF:
                     messages = ring.tile([P, CRYSTALS, PER_CRYSTAL], F32, name="messages")
@@ -138,14 +155,19 @@ def tile_crystalencoder_kernel(tc, table, cart, edge_w, edge_b, node_w, node_b, 
                             minus_gates[n][:, r, first : first + PER_CRYSTAL],
                             ALU.mult,
                         )
-                    nc.tensor.matmul(sums_from(PER_CRYSTAL - t, t), identity[:], messages[:], start=False, stop=False)
+                    add_to_sums(messages, PER_CRYSTAL - t, t)
 
         n_batches = len(pieces) // BATCH
         batch_pieces = [list(range(b * BATCH, (b + 1) * BATCH)) for b in range(n_batches)]
         batch_pieces[-1].extend(range(n_batches * BATCH, len(pieces)))
 
+        def finish(members):
+            for n in members:
+                repeat_ends(n)
+            for n in members:
+                send_turned(n)
+
         minus_wx = {n: make_minus_wx(n) for n in batch_pieces[0]}
-        made = None
         for b, members in enumerate(batch_pieces):
             sigmoid = batches.tile([P, (BATCH + 1) * PIECE * ATOMS], F32, name="sigmoid")
             spans = {}
@@ -155,6 +177,8 @@ def tile_crystalencoder_kernel(tc, table, cart, edge_w, edge_b, node_w, node_b, 
             if b + 1 < n_batches:
                 for n in batch_pieces[b + 1]:
                     minus_wx[n] = make_minus_wx(n)
+            if b > 0:
+                finish(batch_pieces[b - 1])
             for n in members:
                 width = len(pieces[n]) * ATOMS
                 log_part = logs.tile([P, PIECE * ATOMS], F32, name="log_part")
@@ -167,19 +191,9 @@ def tile_crystalencoder_kernel(tc, table, cart, edge_w, edge_b, node_w, node_b, 
                     ALU.add,
                     ALU.min,
                 )
-                reach = max([t for t in pieces[n] if t < HALF] + [0])
-                if reach > 0:
-                    nc.scalar.copy(
-                        minus_gates[n][:, :, FIRST[0] - reach : FIRST[0]], minus_gates[n][:, :, FIRST[1] - reach : FIRST[1]]
-                    )
-                    nc.scalar.copy(
-                        minus_gates[n][:, :, FIRST[1] + PER_CRYSTAL : FIRST[1] + PER_CRYSTAL + reach],
-                        minus_gates[n][:, :, FIRST[1] : FIRST[1] + reach],
-                    )
-                if made is not None:
-                    send_piece(made)
-                made = n
-        send_piece(made)
+            for n in members:
+                send_computed(n)
+        finish(batch_pieces[-1])
 
         agg = held.tile([P, CRYSTALS, PER_CRYSTAL], BF16, name="agg")
         with nc.allow_low_precision(reason="agg is rounded to bfloat16 for the matmul with node_w"):

@@ -19,7 +19,7 @@ GAMMA = 1.0 / 64.0
 EPS = 1e-6
 STEPS = HALF + 1
 PIECE = 4
-BATCH = 2
+BATCHES = (2, 3, 4)
 BANK = 512
 FLOOR = 2.0**-60
 
@@ -31,10 +31,10 @@ def tile_crystalencoder_kernel(tc, table, cart, edge_w, edge_b, node_w, node_b, 
     with (
         tc.tile_pool(name="held", bufs=1) as held,
         tc.tile_pool(name="batches", bufs=2) as batches,
-        tc.tile_pool(name="logs", bufs=4) as logs,
+        tc.tile_pool(name="logs", bufs=8) as logs,
         tc.tile_pool(name="ring", bufs=8) as ring,
         tc.psum_pool(name="psum", bufs=1) as psum,
-        tc.psum_pool(name="banks", bufs=4) as banks,
+        tc.psum_pool(name="banks", bufs=6) as banks,
     ):
         identity = held.tile([P, P], F32, name="identity")
         make_identity(nc, identity[:])
@@ -157,9 +157,9 @@ def tile_crystalencoder_kernel(tc, table, cart, edge_w, edge_b, node_w, node_b, 
                         )
                     add_to_sums(messages, PER_CRYSTAL - t, t)
 
-        n_batches = len(pieces) // BATCH
-        batch_pieces = [list(range(b * BATCH, (b + 1) * BATCH)) for b in range(n_batches)]
-        batch_pieces[-1].extend(range(n_batches * BATCH, len(pieces)))
+        assert sum(BATCHES) == len(pieces)
+        n_batches = len(BATCHES)
+        batch_pieces = [list(range(sum(BATCHES[:b]), sum(BATCHES[: b + 1]))) for b in range(n_batches)]
 
         def finish(members):
             for n in members:
@@ -169,7 +169,7 @@ def tile_crystalencoder_kernel(tc, table, cart, edge_w, edge_b, node_w, node_b, 
 
         minus_wx = {n: make_minus_wx(n) for n in batch_pieces[0]}
         for b, members in enumerate(batch_pieces):
-            sigmoid = batches.tile([P, (BATCH + 1) * PIECE * ATOMS], F32, name="sigmoid")
+            sigmoid = batches.tile([P, max(BATCHES) * PIECE * ATOMS], F32, name="sigmoid")
             spans = {}
             for place, n in enumerate(members):
                 spans[n] = slice(place * PIECE * ATOMS, place * PIECE * ATOMS + len(pieces[n]) * ATOMS)

@@ -78,9 +78,12 @@ def tile_crystalencoder_kernel(tc, table, cart, edge_w, edge_b, node_w, node_b, 
         sums = psum.tile([P, BANK], F32, name="sums")
         nc.tensor.matmul(sums[:, 0 : CRYSTALS * ATOMS], identity[:], zeros[:], start=True, stop=False)
 
+        def two_windows(flat, first0, first1):
+            apart = first1 - first0
+            return flat[:, first0 : first0 + 2 * apart].rearrange("p (c n) -> p c n", c=2)[:, :, 0:PER_CRYSTAL]
+
         def sums_from(s0, s1):
-            apart = ATOMS + s1 - s0
-            return sums[:, s0 : s0 + CRYSTALS * apart].rearrange("p (c n) -> p c n", c=CRYSTALS)[:, :, 0:PER_CRYSTAL]
+            return two_windows(sums, s0, ATOMS + s1)
 
         diff = held.tile([P, DIMS, PER_CRYSTAL], F32, name="diff")
         nc.vector.tensor_tensor(
@@ -110,11 +113,19 @@ def tile_crystalencoder_kernel(tc, table, cart, edge_w, edge_b, node_w, node_b, 
             return minus_wx
 
 
+        ROW = HALF + ATOMS + HALF
         FIRST = (HALF, HALF + PER_CRYSTAL)
+        gates_flat = [
+            held.tile([P, len(steps) * ROW + PER_CRYSTAL], F32, name=f"minus_gates{n}") for n, steps in enumerate(pieces)
+        ]
         minus_gates = [
-            held.tile([P, len(steps), HALF + ATOMS + HALF], F32, name=f"minus_gates{n}") for n, steps in enumerate(pieces)
+            gates_flat[n][:, 0 : len(steps) * ROW].rearrange("p (r w) -> p r w", w=ROW) for n, steps in enumerate(pieces)
         ]
         per_crystal_columns = PER_CRYSTAL // 16
+
+        assert sum(BATCHES) == len(pieces)
+        n_batches = len(BATCHES)
+        batch_pieces = [list(range(sum(BATCHES[:b]), sum(BATCHES[: b + 1]))) for b in range(n_batches)]
 
         sent = []
 
@@ -144,26 +155,46 @@ def tile_crystalencoder_kernel(tc, table, cart, edge_w, edge_b, node_w, node_b, 
                     minus_gates[n][:, :, FIRST[1] : FIRST[1] + reach],
                 )
 
+        side_by_side = {
+            n: held.tile([P, len(pieces[n]), ATOMS], F32, name=f"side_by_side{n}")
+            for members in batch_pieces[1:]
+            for n in members
+            if pieces[n][0] < HALF
+        }
+
+        def copy_turned(n):
+            for r, t in enumerate(pieces[n]):
+                if n in side_by_side and 0 < t < HALF:
+                    nc.scalar.copy(
+                        side_by_side[n][:, r, :].rearrange("p (c j) -> p c j", c=CRYSTALS),
+                        two_windows(gates_flat[n], r * ROW + FIRST[0] - t, r * ROW + FIRST[1] + t),
+                    )
+
         def send_turned(n):
             for r, t in enumerate(pieces[n]):
                 if 0 < t < HALF:
                     messages = ring.tile([P, CRYSTALS, PER_CRYSTAL], F32, name="messages")
-                    for c, first in enumerate((FIRST[0] - t, FIRST[1] + t)):
+                    if n in side_by_side:
                         nc.vector.tensor_tensor(
-                            messages[:, c, :],
-                            table_sb[:].indirect(offsets[:, c * per_crystal_columns : (c + 1) * per_crystal_columns]),
-                            minus_gates[n][:, r, first : first + PER_CRYSTAL],
+                            messages[:].rearrange("p c j -> p (c j)"),
+                            table_sb[:].indirect(offsets[:]),
+                            side_by_side[n][:, r, :],
                             ALU.mult,
                         )
+                    else:
+                        for c, first in enumerate((FIRST[0] - t, FIRST[1] + t)):
+                            nc.vector.tensor_tensor(
+                                messages[:, c, :],
+                                table_sb[:].indirect(offsets[:, c * per_crystal_columns : (c + 1) * per_crystal_columns]),
+                                minus_gates[n][:, r, first : first + PER_CRYSTAL],
+                                ALU.mult,
+                            )
                     add_to_sums(messages, PER_CRYSTAL - t, t)
-
-        assert sum(BATCHES) == len(pieces)
-        n_batches = len(BATCHES)
-        batch_pieces = [list(range(sum(BATCHES[:b]), sum(BATCHES[: b + 1]))) for b in range(n_batches)]
 
         def finish(members):
             for n in members:
                 repeat_ends(n)
+                copy_turned(n)
             for n in members:
                 send_turned(n)
 

@@ -60,10 +60,14 @@ def tile_crystalencoder_kernel(tc, table, cart, edge_w, edge_b, node_w, node_b, 
         node_b_sb = held.tile([P, 1], F32, name="node_b_sb")
         nc.gpsimd.dma_start(node_b_sb[:], node_b)
 
-        shift_mask = held.tile([P, CRYSTALS, 2 * PER_CRYSTAL], F32, name="shift_mask")
-        identity_by_crystal = identity[:].rearrange("p (c n) -> p c n", c=CRYSTALS)
-        nc.vector.tensor_copy(shift_mask[:, :, 0:PER_CRYSTAL], identity_by_crystal)
-        nc.vector.tensor_copy(shift_mask[:, :, PER_CRYSTAL:], identity_by_crystal)
+        def two_windows(flat, first0, first1):
+            apart = first1 - first0
+            return flat[:, first0 : first0 + 2 * apart].rearrange("p (c n) -> p c n", c=2)[:, :, 0:PER_CRYSTAL]
+
+        shift_mask = held.tile([P, (CRYSTALS + 1) * ATOMS], F32, name="shift_mask")
+        twice = shift_mask[:, 0 : CRYSTALS * ATOMS].rearrange("p (c h n) -> p c h n", c=CRYSTALS, h=2)
+        for h in range(2):
+            nc.vector.tensor_copy(twice[:, :, h, :], identity[:].rearrange("p (c n) -> p c n", c=CRYSTALS))
         zeros = held.tile([P, CRYSTALS * ATOMS], F32, name="zeros")
         nc.vector.memset(zeros[:], 0.0)
         eps_bias = held.tile([P, 1], F32, name="eps_bias")
@@ -77,10 +81,6 @@ def tile_crystalencoder_kernel(tc, table, cart, edge_w, edge_b, node_w, node_b, 
 
         sums = psum.tile([P, BANK], F32, name="sums")
         nc.tensor.matmul(sums[:, 0 : CRYSTALS * ATOMS], identity[:], zeros[:], start=True, stop=False)
-
-        def two_windows(flat, first0, first1):
-            apart = first1 - first0
-            return flat[:, first0 : first0 + 2 * apart].rearrange("p (c n) -> p c n", c=2)[:, :, 0:PER_CRYSTAL]
 
         def sums_from(s0, s1):
             return two_windows(sums, s0, ATOMS + s1)
@@ -97,12 +97,14 @@ def tile_crystalencoder_kernel(tc, table, cart, edge_w, edge_b, node_w, node_b, 
         nc.scalar.activation(rbf[:], dist2[:], ACT.Exp, bias=eps_bias[:], scale=-GAMMA)
 
         pieces = [range(first, min(first + PIECE, STEPS)) for first in range(0, STEPS, PIECE)]
+        rbf_both = rbf[:].unsqueeze(1).to_broadcast([P, CRYSTALS, PER_CRYSTAL])
         picked = []
         for n, steps in enumerate(pieces):
             picked.append(held.tile([P, len(steps), CRYSTALS, PER_CRYSTAL], F32, name=f"picked{n}"))
             for r, t in enumerate(steps):
-                for c, s in enumerate((t, PER_CRYSTAL - t)):
-                    nc.vector.tensor_tensor(picked[n][:, r, c, :], rbf[:], shift_mask[:, c, s : s + PER_CRYSTAL], ALU.mult)
+                nc.vector.tensor_tensor(
+                    picked[n][:, r, :, :], rbf_both, two_windows(shift_mask, t, ATOMS + PER_CRYSTAL - t), ALU.mult
+                )
 
         def make_minus_wx(n):
             bank = banks.tile([P, PIECE * ATOMS], F32, name="bank")

import concourse.mybir as mybir
from concourse.masks import make_identity

F32 = mybir.dt.float32
BF16 = mybir.dt.bfloat16
U16 = mybir.dt.uint16
ACT = mybir.ActivationFunctionType
ALU = mybir.AluOpType
AXIS = mybir.AxisListType

P = 128
TYPES = 256
ATOMS = 128
CRYSTALS = 2
PER_CRYSTAL = ATOMS // CRYSTALS
HALF = PER_CRYSTAL // 2
DIMS = 3
GAMMA = 1.0 / 64.0
EPS = 1e-6
STEPS = HALF + 1
PIECE = 4
BATCHES = (2, 3, 4)
BANK = 512
FLOOR = 2.0**-60

FLOPS = 2 * P * P * ATOMS


def tile_crystalencoder_kernel(tc, table, cart, edge_w, edge_b, node_w, node_b, offs, out):
    nc = tc.nc
    with (
        tc.tile_pool(name="held", bufs=1) as held,
        tc.tile_pool(name="batches", bufs=2) as batches,
        tc.tile_pool(name="logs", bufs=8) as logs,
        tc.tile_pool(name="ring", bufs=8) as ring,
        tc.psum_pool(name="psum", bufs=1) as psum,
        tc.psum_pool(name="banks", bufs=6) as banks,
    ):
        identity = held.tile([P, P], F32, name="identity")
        make_identity(nc, identity[:])
        halves = [slice(c * PER_CRYSTAL, (c + 1) * PER_CRYSTAL) for c in range(CRYSTALS)]
        cart_crystal = held.tile([P, DIMS, PER_CRYSTAL], F32, name="cart_crystal")
        for own, queue in zip(halves, (nc.sync, nc.scalar)):
            queue.dma_start(
                cart_crystal[own, :, :], cart[:, own].unsqueeze(0).to_broadcast([PER_CRYSTAL, DIMS, PER_CRYSTAL])
            )
        cart_own = held.tile([P, DIMS], F32, name="cart_own")
        with nc.allow_non_contiguous_dma(reason="three coordinates to a partition"):
            nc.sync.dma_start(cart_own[:], cart.rearrange("d n -> n d"))
        w_rows = held.tile([P, P], F32, name="w_rows")
        nc.sync.dma_start(w_rows[:], edge_w.rearrange("c o -> (c o)").partition_broadcast(P))
        edge_b_sb = held.tile([P, 1], F32, name="edge_b_sb")
        nc.scalar.dma_start(edge_b_sb[:], edge_b)
        offsets = held.tile([P, ATOMS // 16], U16, name="offsets")
        nc.sync.dma_start(offsets[:], offs)
        table_sb = held.tile([P, TYPES], F32, name="table_sb")
        nc.sync.dma_start(table_sb[:], table)
        node_w_sb = held.tile([P, P], BF16, name="node_w_sb")
        nc.gpsimd.dma_start(node_w_sb[:], node_w)
        node_b_sb = held.tile([P, 1], F32, name="node_b_sb")
        nc.gpsimd.dma_start(node_b_sb[:], node_b)

        def two_windows(flat, first0, first1):
            apart = first1 - first0
            return flat[:, first0 : first0 + 2 * apart].rearrange("p (c n) -> p c n", c=2)[:, :, 0:PER_CRYSTAL]

        shift_mask = held.tile([P, (CRYSTALS + 1) * ATOMS], F32, name="shift_mask")
        twice = shift_mask[:, 0 : CRYSTALS * ATOMS].rearrange("p (c h n) -> p c h n", c=CRYSTALS, h=2)
        for h in range(2):
            nc.vector.tensor_copy(twice[:, :, h, :], identity[:].rearrange("p (c n) -> p c n", c=CRYSTALS))
        zeros = held.tile([P, CRYSTALS * ATOMS], F32, name="zeros")
        nc.vector.memset(zeros[:], 0.0)
        eps_bias = held.tile([P, 1], F32, name="eps_bias")
        nc.vector.memset(eps_bias[:], -GAMMA * EPS)
        minus_b = held.tile([P, 1], F32, name="minus_b")
        nc.vector.tensor_scalar_mul(minus_b[:], edge_b_sb[:], -1.0)
        minus_w_rows = held.tile([P, P], F32, name="minus_w_rows")
        nc.gpsimd.tensor_scalar_mul(minus_w_rows[:], w_rows[:], -1.0)
        minus_node_w = held.tile([P, P], BF16, name="minus_node_w")
        nc.gpsimd.tensor_scalar_mul(minus_node_w[:], node_w_sb[:], -1.0)

        sums = psum.tile([P, BANK], F32, name="sums")
        nc.tensor.matmul(sums[:, 0 : CRYSTALS * ATOMS], identity[:], zeros[:], start=True, stop=False)

        def sums_from(s0, s1):
            return two_windows(sums, s0, ATOMS + s1)

        diff = held.tile([P, DIMS, PER_CRYSTAL], F32, name="diff")
        nc.vector.tensor_tensor(
            diff[:], cart_crystal[:], cart_own[:].unsqueeze(2).to_broadcast([P, DIMS, PER_CRYSTAL]), ALU.subtract
        )
        square = held.tile([P, DIMS, PER_CRYSTAL], F32, name="square")
        nc.vector.tensor_tensor(square[:], diff[:], diff[:], ALU.mult)
        dist2 = held.tile([P, PER_CRYSTAL], F32, name="dist2")
        nc.vector.tensor_reduce(dist2[:], square[:].rearrange("p d n -> p n d"), AXIS.X, ALU.add)
        rbf = held.tile([P, PER_CRYSTAL], F32, name="rbf")
        nc.scalar.activation(rbf[:], dist2[:], ACT.Exp, bias=eps_bias[:], scale=-GAMMA)

        pieces = [range(first, min(first + PIECE, STEPS)) for first in range(0, STEPS, PIECE)]
        rbf_both = rbf[:].unsqueeze(1).to_broadcast([P, CRYSTALS, PER_CRYSTAL])
        picked = []
        for n, steps in enumerate(pieces):
            picked.append(held.tile([P, len(steps), CRYSTALS, PER_CRYSTAL], F32, name=f"picked{n}"))
            for r, t in enumerate(steps):
                nc.vector.tensor_tensor(
                    picked[n][:, r, :, :], rbf_both, two_windows(shift_mask, t, ATOMS + PER_CRYSTAL - t), ALU.mult
                )

        def make_minus_wx(n):
            bank = banks.tile([P, PIECE * ATOMS], F32, name="bank")
            minus_wx = bank[:, 0 : len(pieces[n]) * ATOMS]
            nc.tensor.matmul(
                minus_wx, minus_w_rows[:], picked[n][:].rearrange("p r c j -> p (r c j)"), start=True, stop=True
            )
            return minus_wx


        ROW = HALF + ATOMS + HALF
        FIRST = (HALF, HALF + PER_CRYSTAL)
        gates_flat = [
            held.tile([P, len(steps) * ROW + PER_CRYSTAL], F32, name=f"minus_gates{n}") for n, steps in enumerate(pieces)
        ]
        minus_gates = [
            gates_flat[n][:, 0 : len(steps) * ROW].rearrange("p (r w) -> p r w", w=ROW) for n, steps in enumerate(pieces)
        ]
        per_crystal_columns = PER_CRYSTAL // 16

        assert sum(BATCHES) == len(pieces)
        n_batches = len(BATCHES)
        batch_pieces = [list(range(sum(BATCHES[:b]), sum(BATCHES[: b + 1]))) for b in range(n_batches)]

        sent = []

        def add_to_sums(messages, s0, s1):
            sent.append((s0, s1))
            nc.tensor.matmul(sums_from(s0, s1), identity[:], messages[:], start=False, stop=(len(sent) == PER_CRYSTAL))

        def send_computed(n):
            for r, t in enumerate(pieces[n]):
                messages = ring.tile([P, CRYSTALS, PER_CRYSTAL], F32, name="messages")
                nc.vector.tensor_tensor(
                    messages[:].rearrange("p c j -> p (c j)"),
                    table_sb[:].indirect(offsets[:]),
                    minus_gates[n][:, r, HALF : HALF + ATOMS],
                    ALU.mult,
                )
                add_to_sums(messages, t, PER_CRYSTAL - t)

        def repeat_ends(n):
            reach = max([t for t in pieces[n] if t < HALF] + [0])
            if reach > 0:
                nc.scalar.copy(
                    minus_gates[n][:, :, FIRST[0] - reach : FIRST[0]], minus_gates[n][:, :, FIRST[1] - reach : FIRST[1]]
                )
                nc.scalar.copy(
                    minus_gates[n][:, :, FIRST[1] + PER_CRYSTAL : FIRST[1] + PER_CRYSTAL + reach],
                    minus_gates[n][:, :, FIRST[1] : FIRST[1] + reach],
                )

        side_by_side = {
            n: held.tile([P, len(pieces[n]), ATOMS], F32, name=f"side_by_side{n}")
            for members in batch_pieces[1:]
            for n in members
            if pieces[n][0] < HALF
        }

        def copy_turned(n):
            for r, t in enumerate(pieces[n]):
                if n in side_by_side and 0 < t < HALF:
                    nc.scalar.copy(
                        side_by_side[n][:, r, :].rearrange("p (c j) -> p c j", c=CRYSTALS),
                        two_windows(gates_flat[n], r * ROW + FIRST[0] - t, r * ROW + FIRST[1] + t),
                    )

        def send_turned(n):
            for r, t in enumerate(pieces[n]):
                if 0 < t < HALF:
                    messages = ring.tile([P, CRYSTALS, PER_CRYSTAL], F32, name="messages")
                    if n in side_by_side:
                        nc.vector.tensor_tensor(
                            messages[:].rearrange("p c j -> p (c j)"),
                            table_sb[:].indirect(offsets[:]),
                            side_by_side[n][:, r, :],
                            ALU.mult,
                        )
                    else:
                        for c, first in enumerate((FIRST[0] - t, FIRST[1] + t)):
                            nc.vector.tensor_tensor(
                                messages[:, c, :],
                                table_sb[:].indirect(offsets[:, c * per_crystal_columns : (c + 1) * per_crystal_columns]),
                                minus_gates[n][:, r, first : first + PER_CRYSTAL],
                                ALU.mult,
                            )
                    add_to_sums(messages, PER_CRYSTAL - t, t)

        def finish(members):
            for n in members:
                repeat_ends(n)
                copy_turned(n)
            for n in members:
                send_turned(n)

        minus_wx = {n: make_minus_wx(n) for n in batch_pieces[0]}
        for b, members in enumerate(batch_pieces):
            sigmoid = batches.tile([P, max(BATCHES) * PIECE * ATOMS], F32, name="sigmoid")
            spans = {}
            for place, n in enumerate(members):
                spans[n] = slice(place * PIECE * ATOMS, place * PIECE * ATOMS + len(pieces[n]) * ATOMS)
                nc.scalar.activation(sigmoid[:, spans[n]], minus_wx[n], ACT.Sigmoid, bias=minus_b[:])
            if b + 1 < n_batches:
                for n in batch_pieces[b + 1]:
                    minus_wx[n] = make_minus_wx(n)
            if b > 0:
                finish(batch_pieces[b - 1])
            for n in members:
                width = len(pieces[n]) * ATOMS
                log_part = logs.tile([P, PIECE * ATOMS], F32, name="log_part")
                nc.scalar.activation(log_part[:, 0:width], sigmoid[:, spans[n]], ACT.Ln, bias=FLOOR)
                nc.vector.scalar_tensor_tensor(
                    minus_gates[n][:, :, HALF : HALF + ATOMS],
                    minus_wx[n].rearrange("p (r a) -> p r a", a=ATOMS),
                    minus_b[:],
                    log_part[:, 0:width].rearrange("p (r a) -> p r a", a=ATOMS),
                    ALU.add,
                    ALU.min,
                )
            for n in members:
                send_computed(n)
        finish(batch_pieces[-1])

        agg = held.tile([P, CRYSTALS, PER_CRYSTAL], BF16, name="agg")
        with nc.allow_low_precision(reason="agg is rounded to bfloat16 for the matmul with node_w"):
            nc.vector.tensor_reduce(
                agg[:], sums[:, 0 : CRYSTALS * ATOMS].rearrange("p (c h i) -> p c i h", c=CRYSTALS, h=2), AXIS.X, ALU.add
            )
        projected = psum.tile([P, ATOMS], F32, name="projected")
        nc.tensor.matmul(projected[:], minus_node_w[:], agg[:].rearrange("p c i -> p (c i)"), start=True, stop=True)
        update = held.tile([P, ATOMS], F32, name="update")
        nc.scalar.activation(update[:], projected[:], ACT.Silu, bias=node_b_sb[:])
        result = held.tile([P, ATOMS], F32, name="result")
        nc.vector.tensor_tensor(result[:], table_sb[:].indirect(offsets[:]), update[:], ALU.add)
        nc.sync.dma_start(out, result[:])
